import numpy as np
import ml_dtypes


def mxq(x, axis, fmt="e4m3"):
    dtype, down = {"e4m3": (ml_dtypes.float8_e4m3fn, 7), "e5m2": (ml_dtypes.float8_e5m2, 14)}[fmt]
    v = np.moveaxis(np.asarray(x, np.float32).astype(ml_dtypes.bfloat16).astype(np.float64), axis, -1)
    blocks = v.reshape(v.shape[:-1] + (-1, 32))
    amax = np.abs(blocks).max(-1, keepdims=True)
    byte = np.maximum(np.where(amax > 0, np.frexp(amax)[1] - 1 + 127, 0) - down, 1)
    scale = np.exp2(byte - 127.0)
    codes = (blocks / scale).astype(np.float32).astype(dtype).astype(np.float64)
    return np.moveaxis((codes * scale).reshape(v.shape), -1, axis)


WIDE = False


def mx_kscale(k):
    if not WIDE:
        return np.ones(k)
    levels = np.array([10, -10, 5, -5, 0])
    if k % 512:
        return np.exp2(np.random.permutation(np.resize(levels, k // 32))).repeat(32)
    a = np.empty((k // 512, 16))
    for p in range(k // 512):
        a[p, :8] = np.random.permutation(np.resize(levels, 8))
        for g in range(8):
            far = levels[np.abs(levels - a[p, g]) >= 10]
            a[p, g + 8] = far[np.random.randint(len(far))]
    return np.exp2(a.ravel()).repeat(32)


BF16 = ml_dtypes.bfloat16


def bf(x):
    return np.asarray(x, np.float32).astype(BF16)


def f64(x):
    return np.asarray(x).astype(np.float64)


N, K, F, NB = 4096, 512, 128, 32


def setup_inputs():
    s = mx_kscale(N)
    c = s / s.min()
    r = s.max() / s
    edge = np.random.random_sample((N, N)) < NB / N
    return {"h_ln": bf(np.random.standard_normal((N, F)) * r[:, None]),
            "adj": bf(np.random.random_sample((N, N)) * edge * c[None, :]),
            "W2": bf(np.random.standard_normal((F, F)) * 2.0 / np.sqrt(F)),
            "b2": bf(np.random.standard_normal(F) * 0.2)}


def reference(h_ln, adj, W2, b2):
    a = f64(adj)
    h = f64(h_ln) @ f64(W2) + f64(b2)
    deg = a.sum(axis=1) + 1.0
    dinv = np.where(deg > 0, deg ** -0.5, 0.0)
    hs = dinv[:, None] * h
    agg = (mxq(a, 1, "e4m3") @ mxq(hs, 0, "e4m3")) + hs
    return dinv[:, None] * agg

@@ -1,0 +1,236 @@
+import concourse.mybir as mybir
+from concourse.masks import make_identity
+
+F32 = mybir.dt.float32
+BF16 = mybir.dt.bfloat16
+U32 = mybir.dt.uint32
+U8 = mybir.dt.uint8
+FP8X4 = mybir.dt.float8_e4m3fn_x4
+ALU = mybir.AluOpType
+ACT = mybir.ActivationFunctionType
+
+P = 128
+NODES = 4096
+FEATS = 128
+TILES = NODES // P
+PACK = 4
+K_PASS = P * PACK
+PASSES = NODES // K_PASS
+BANK = 512
+PASSES_IN_BANK = BANK // (2 * P)
+BANKS_IN_TILE = PASSES // PASSES_IN_BANK
+TILES_IN_BANK = BANK // FEATS
+FEATURE_GROUP = 8
+
+TENSOR_SUM_PASSES = 4
+TENSOR_SUM_COLS = TENSOR_SUM_PASSES * K_PASS
+ROWS_IN_CHUNK = P // PACK
+CHUNKS = P // ROWS_IN_CHUNK
+
+SMALLEST_DEG = 2.0**-100
+
+FLOPS = 2 * NODES * NODES * FEATS + 2 * NODES * FEATS * FEATS
+
+
+def tile_gcnlayer_pb_t_kernel(tc, h_ln, adj, W2, b2, out):
+    nc = tc.nc
+
+    adj_tiles = adj.rearrange("(g p e) j -> p g e j", p=P, e=PACK)
+    h_ln_spans = h_ln.rearrange("(g p e) k -> p g (e k)", p=P, e=PACK)
+    out_spans = out.rearrange("(g p e) f -> p g (e f)", p=P, e=PACK)
+
+    with tc.tile_pool(name="keep", bufs=1) as keep, tc.psum_pool(name="psum", bufs=8) as psum:
+        ident_f32 = keep.tile([P, P], F32)
+        make_identity(nc, ident_f32[:])
+        ident_bf16 = keep.tile([P, P], BF16)
+        make_identity(nc, ident_bf16[:])
+        w2_sb = keep.tile([FEATS, FEATS], BF16)
+        nc.scalar.dma_start(out=w2_sb[:], in_=W2)
+        ones = keep.tile([P, P], BF16)
+        nc.vector.memset(ones[:], 1.0)
+        bias_rows = keep.tile([P, FEATS], BF16)
+        nc.vector.memset(bias_rows[:], 0.0)
+        nc.scalar.dma_start(out=bias_rows[0:1, :], in_=b2.rearrange("(o f) -> o f", o=1))
+        fold = keep.tile([P, CHUNKS, P], F32)
+        nc.vector.memset(fold[:], 0.0)
+        for chunk in range(CHUNKS):
+            nc.vector.tensor_reduce(
+                out=fold[:, chunk, chunk * ROWS_IN_CHUNK : (chunk + 1) * ROWS_IN_CHUNK],
+                in_=ident_f32[:].rearrange("k (i t) -> k i t", t=PACK),
+                axis=mybir.AxisListType.X,
+                op=ALU.add,
+            )
+        table_warmer = keep.tile([P, 1], F32)
+        nc.vector.memset(table_warmer[:], 1.0)
+        nc.scalar.activation(out=table_warmer[:], in_=table_warmer[:], func=ACT.Sqrt)
+
+        adj_codes = keep.tile([P, TILES, PASSES * P], U32, align_bytes=64)
+        adj_scales = keep.tile([P, TILES, PASSES * P], U8, align_bytes=64)
+        h_lnT = keep.tile([FEATS, NODES], BF16)
+        sums_vector = keep.tile([P, TILES], F32)
+        sums_tensor = psum.tile([P, CHUNKS * TILES], F32, tag="bank")
+
+        with tc.tile_pool(name="stream", bufs=1) as stream:
+            unread = stream.tile([P, NODES - TENSOR_SUM_COLS], BF16)
+            turned = {}
+            for s in range(TILES + 1):
+                if s < TILES:
+                    rows = stream.tile([P, NODES], BF16, tag="rows", bufs=4)
+                    nc.sync.dma_start(out=rows[:], in_=adj_tiles[:, s // PACK, s % PACK, :])
+
+                    nc.vector.tensor_scalar(
+                        out=unread[:],
+                        in0=rows[:, TENSOR_SUM_COLS:],
+                        scalar1=1.0,
+                        scalar2=None,
+                        op0=ALU.mult,
+                        op1=ALU.add,
+                        accum_out=sums_vector[:, s : s + 1],
+                    )
+
+                    place = s % FEATURE_GROUP
+                    if place == 0:
+                        features = stream.tile([P, FEATURE_GROUP * FEATS], BF16, tag="features", bufs=2)
+                        first_span = s // PACK
+                        nc.sync.dma_start(
+                            out=features[:].rearrange("p (g x) -> p g x", x=PACK * FEATS),
+                            in_=h_ln_spans[:, first_span : first_span + FEATURE_GROUP // PACK, :],
+                        )
+                        features_bank = psum.tile([FEATS, FEATURE_GROUP * P], BF16, tag="bank")
+                    nc.tensor.transpose(
+                        features_bank[:, place * P : (place + 1) * P],
+                        features[:, place * FEATS : (place + 1) * FEATS],
+                        ident_bf16[:],
+                    )
+                    if place == FEATURE_GROUP - 1:
+                        nc.scalar.copy(
+                            out=h_lnT[:, (s - place) * P : (s + 1) * P], in_=features_bank[:]
+                        )
+
+                    row_words = rows[:].bitcast(F32)
+                    grouped = stream.tile([P, NODES], BF16, tag="grouped", bufs=2, align_bytes=64)
+                    grouped_words = grouped[:].bitcast(F32).rearrange(
+                        "q (c i u) -> q c i u", c=PASSES, u=2
+                    )
+                    for b in range(BANKS_IN_TILE):
+                        bank = psum.tile([P, BANK], F32, tag="bank")
+                        for half in range(2 * PASSES_IN_BANK):
+                            c, u = b * PASSES_IN_BANK + half // 2, half % 2
+                            nc.tensor.transpose(
+                                bank[:, half * P : (half + 1) * P],
+                                row_words[:, 2 * P * c + u : 2 * P * (c + 1) : 2],
+                                ident_f32[:],
+                            )
+                        nc.scalar.copy(
+                            out=grouped_words[:, b * PASSES_IN_BANK : (b + 1) * PASSES_IN_BANK, :, :],
+                            in_=bank[:].rearrange("q (c u i) -> q c i u", c=PASSES_IN_BANK, u=2),
+                        )
+                    turned[s] = grouped
+                if s >= 1:
+                    for chunk in range(CHUNKS):
+                        for c in range(TENSOR_SUM_PASSES):
+                            first_col = (c * P + chunk * ROWS_IN_CHUNK) * PACK
+                            nc.tensor.matmul(
+                                sums_tensor[:, chunk * TILES + s - 1 : chunk * TILES + s],
+                                lhsT=turned[s - 1][:, first_col : first_col + P],
+                                rhs=ones[:, 0:1],
+                                start=(c == 0),
+                                stop=(c == TENSOR_SUM_PASSES - 1),
+                            )
+                    nc.vector.quantize_mx(
+                        out=adj_codes[:, s - 1, :].bitcast(FP8X4),
+                        scales=adj_scales[:, s - 1, :],
+                        in_=turned[s - 1][:],
+                    )
+
+        with tc.tile_pool(name="tail", bufs=1) as tail:
+            sums_by_value = tail.tile([P, CHUNKS * TILES], F32)
+            nc.vector.tensor_copy(out=sums_by_value[:], in_=sums_tensor[:])
+            folded_bank = psum.tile([P, BANK], F32, tag="bank")
+            folded = folded_bank[:, :TILES]
+            for chunk in range(CHUNKS):
+                nc.tensor.matmul(
+                    folded,
+                    lhsT=fold[:, chunk, :],
+                    rhs=sums_by_value[:, chunk * TILES : (chunk + 1) * TILES],
+                    start=(chunk == 0),
+                    stop=(chunk == CHUNKS - 1),
+                )
+            deg = tail.tile([P, TILES], F32)
+            nc.vector.scalar_tensor_tensor(
+                out=deg[:], in0=folded, scalar=1.0, in1=sums_vector[:], op0=ALU.add, op1=ALU.add
+            )
+            root = tail.tile([P, TILES], F32)
+            nc.vector.tensor_scalar_max(out=root[:], in0=deg[:], scalar1=SMALLEST_DEG)
+            nc.scalar.activation(out=root[:], in_=root[:], func=ACT.Sqrt)
+            one_over_root = tail.tile([P, TILES], F32)
+            nc.vector.reciprocal(out=one_over_root[:], in_=root[:])
+            dinv = tail.tile([P, TILES], F32)
+            nc.vector.scalar_tensor_tensor(
+                out=dinv[:], in0=deg[:], scalar=0.0, in1=one_over_root[:], op0=ALU.is_gt, op1=ALU.mult
+            )
+            dinv_squared = tail.tile([P, TILES], F32)
+            nc.vector.tensor_mul(out=dinv_squared[:], in0=dinv[:], in1=dinv[:])
+
+            hs_grouped = tail.tile([P, PASSES, FEATS * PACK], BF16, align_bytes=64)
+            self_term = tail.tile([P, TILES * FEATS], F32)
+            for c in range(PASSES):
+                h_bank = psum.tile([P, BANK], F32, tag="bank")
+                for t in range(PACK):
+                    s = PACK * c + t
+                    h_tile = h_bank[:, t * FEATS : (t + 1) * FEATS]
+                    nc.tensor.matmul(h_tile, lhsT=ones[:], rhs=bias_rows[:], start=True, stop=False)
+                    nc.tensor.matmul(
+                        h_tile, lhsT=h_lnT[:, s * P : (s + 1) * P], rhs=w2_sb[:], start=False, stop=True
+                    )
+                nc.vector.tensor_tensor(
+                    out=hs_grouped[:, c, :].rearrange("q (f t) -> q f t", t=PACK),
+                    in0=h_bank[:].rearrange("q (t f) -> q f t", t=PACK),
+                    in1=dinv[:, PACK * c : PACK * (c + 1)].unsqueeze(1).to_broadcast([P, FEATS, PACK]),
+                    op=ALU.mult,
+                )
+                for t in range(PACK):
+                    s = PACK * c + t
+                    nc.scalar.activation(
+                        out=self_term[:, s * FEATS : (s + 1) * FEATS],
+                        in_=h_bank[:, t * FEATS : (t + 1) * FEATS],
+                        func=ACT.Copy,
+                        scale=dinv_squared[:, s : s + 1],
+                    )
+            hs_codes = tail.tile([P, PASSES * FEATS], U32, align_bytes=64)
+            hs_scales = tail.tile([P, PASSES * FEATS], U8, align_bytes=64)
+            nc.vector.quantize_mx(
+                out=hs_codes[:].bitcast(FP8X4),
+                scales=hs_scales[:],
+                in_=hs_grouped[:].rearrange("q c x -> q (c x)"),
+            )
+
+            for first in range(0, TILES, TILES_IN_BANK):
+                agg_bank = psum.tile([P, BANK], F32, tag="bank")
+                for place in range(TILES_IN_BANK):
+                    s = first + place
+                    for c in range(PASSES):
+                        nc.tensor.matmul_mx(
+                            out=agg_bank[:, place * FEATS : (place + 1) * FEATS],
+                            lhsT=adj_codes[:, s, c * P : (c + 1) * P].bitcast(FP8X4),
+                            lhsT_scale=adj_scales[:, s, c * P : (c + 1) * P],
+                            rhs=hs_codes[:, c * FEATS : (c + 1) * FEATS].bitcast(FP8X4),
+                            rhs_scale=hs_scales[:, c * FEATS : (c + 1) * FEATS],
+                            start=(c == 0),
+                            stop=(c == PASSES - 1),
+                        )
+                result = tail.tile([P, BANK], F32, tag="result", bufs=3)
+                for place in range(TILES_IN_BANK):
+                    s = first + place
+                    nc.vector.scalar_tensor_tensor(
+                        out=result[:, place * FEATS : (place + 1) * FEATS],
+                        in0=agg_bank[:, place * FEATS : (place + 1) * FEATS],
+                        scalar=dinv[:, s : s + 1],
+                        in1=self_term[:, s * FEATS : (s + 1) * FEATS],
+                        op0=ALU.mult,
+                        op1=ALU.add,
+                    )
+                nc.sync.dma_start(
+                    out=out_spans[:, first // PACK, :],
+                    in_=result[:],
+                )

@@ -22,8 +22,9 @@ BANKS_IN_TILE = PASSES // PASSES_IN_BANK
 TILES_IN_BANK = BANK // FEATS
 FEATURE_GROUP = 8
 
-TENSOR_SUM_PASSES = 4
-TENSOR_SUM_COLS = TENSOR_SUM_PASSES * K_PASS
+HALVES = 2
+WORDS_IN_HALF = NODES // (2 * HALVES)
+PASSES_IN_HALF = PASSES // HALVES
 ROWS_IN_CHUNK = P // PACK
 CHUNKS = P // ROWS_IN_CHUNK
 
@@ -67,26 +68,24 @@ def tile_gcnlayer_pb_t_kernel(tc, h_ln, adj, W2, b2, out):
         adj_codes = keep.tile([P, TILES, PASSES * P], U32, align_bytes=64)
         adj_scales = keep.tile([P, TILES, PASSES * P], U8, align_bytes=64)
         h_lnT = keep.tile([FEATS, NODES], BF16)
-        sums_vector = keep.tile([P, TILES], F32)
         sums_tensor = psum.tile([P, CHUNKS * TILES], F32, tag="bank")
 
         with tc.tile_pool(name="stream", bufs=1) as stream:
-            unread = stream.tile([P, NODES - TENSOR_SUM_COLS], BF16)
             turned = {}
             for s in range(TILES + 1):
                 if s < TILES:
-                    rows = stream.tile([P, NODES], BF16, tag="rows", bufs=4)
+                    rows = stream.tile([P, NODES], BF16, tag="rows", bufs=3)
                     nc.sync.dma_start(out=rows[:], in_=adj_tiles[:, s // PACK, s % PACK, :])
 
-                    nc.vector.tensor_scalar(
-                        out=unread[:],
-                        in0=rows[:, TENSOR_SUM_COLS:],
-                        scalar1=1.0,
-                        scalar2=None,
-                        op0=ALU.mult,
-                        op1=ALU.add,
-                        accum_out=sums_vector[:, s : s + 1],
-                    )
+                    paired = stream.tile([P, HALVES, 2, WORDS_IN_HALF // 2], F32, tag="paired", bufs=2)
+                    for half in range(HALVES):
+                        first_word = half * WORDS_IN_HALF
+                        nc.vector.tensor_copy(
+                            out=paired[:, half, :, :],
+                            in_=rows[:]
+                            .bitcast(F32)[:, first_word : first_word + WORDS_IN_HALF]
+                            .rearrange("p (n u) -> p u n", u=2),
+                        )
 
                     place = s % FEATURE_GROUP
                     if place == 0:
@@ -107,18 +106,18 @@ def tile_gcnlayer_pb_t_kernel(tc, h_ln, adj, W2, b2, out):
                             out=h_lnT[:, (s - place) * P : (s + 1) * P], in_=features_bank[:]
                         )
 
-                    row_words = rows[:].bitcast(F32)
                     grouped = stream.tile([P, NODES], BF16, tag="grouped", bufs=2, align_bytes=64)
                     grouped_words = grouped[:].bitcast(F32).rearrange(
                         "q (c i u) -> q c i u", c=PASSES, u=2
                     )
                     for b in range(BANKS_IN_TILE):
                         bank = psum.tile([P, BANK], F32, tag="bank")
-                        for half in range(2 * PASSES_IN_BANK):
-                            c, u = b * PASSES_IN_BANK + half // 2, half % 2
+                        for place in range(2 * PASSES_IN_BANK):
+                            c, u = b * PASSES_IN_BANK + place // 2, place % 2
+                            half, c_in_half = c // PASSES_IN_HALF, c % PASSES_IN_HALF
                             nc.tensor.transpose(
-                                bank[:, half * P : (half + 1) * P],
-                                row_words[:, 2 * P * c + u : 2 * P * (c + 1) : 2],
+                                bank[:, place * P : (place + 1) * P],
+                                paired[:, half, u, c_in_half * P : (c_in_half + 1) * P],
                                 ident_f32[:],
                             )
                         nc.scalar.copy(
@@ -128,14 +127,14 @@ def tile_gcnlayer_pb_t_kernel(tc, h_ln, adj, W2, b2, out):
                     turned[s] = grouped
                 if s >= 1:
                     for chunk in range(CHUNKS):
-                        for c in range(TENSOR_SUM_PASSES):
+                        for c in range(PASSES):
                             first_col = (c * P + chunk * ROWS_IN_CHUNK) * PACK
                             nc.tensor.matmul(
                                 sums_tensor[:, chunk * TILES + s - 1 : chunk * TILES + s],
                                 lhsT=turned[s - 1][:, first_col : first_col + P],
                                 rhs=ones[:, 0:1],
                                 start=(c == 0),
-                                stop=(c == TENSOR_SUM_PASSES - 1),
+                                stop=(c == PASSES - 1),
                             )
                     nc.vector.quantize_mx(
                         out=adj_codes[:, s - 1, :].bitcast(FP8X4),
@@ -157,9 +156,7 @@ def tile_gcnlayer_pb_t_kernel(tc, h_ln, adj, W2, b2, out):
                     stop=(chunk == CHUNKS - 1),
                 )
             deg = tail.tile([P, TILES], F32)
-            nc.vector.scalar_tensor_tensor(
-                out=deg[:], in0=folded, scalar=1.0, in1=sums_vector[:], op0=ALU.add, op1=ALU.add
-            )
+            nc.vector.tensor_scalar_add(out=deg[:], in0=folded, scalar1=1.0)
             root = tail.tile([P, TILES], F32)
             nc.vector.tensor_scalar_max(out=root[:], in0=deg[:], scalar1=SMALLEST_DEG)
             nc.scalar.activation(out=root[:], in_=root[:], func=ACT.Sqrt)

@@ -14,44 +14,69 @@ NODES = 4096
 FEATS = 128
 TILES = NODES // P
 PACK = 4
-K_PASS = P * PACK
-PASSES = NODES // K_PASS
+GROUPS = TILES // PACK
+PASSES = GROUPS
 BANK = 512
-PASSES_IN_BANK = BANK // (2 * P)
-BANKS_IN_TILE = PASSES // PASSES_IN_BANK
-TILES_IN_BANK = BANK // FEATS
-FEATURE_GROUP = 8
-
 HALVES = 2
-WORDS_IN_HALF = NODES // (2 * HALVES)
+HALF = NODES // HALVES
 PASSES_IN_HALF = PASSES // HALVES
+PASSES_IN_BANK = 2
+BANKS_IN_HALF = PASSES_IN_HALF // PASSES_IN_BANK
 ROWS_IN_CHUNK = P // PACK
 CHUNKS = P // ROWS_IN_CHUNK
+SUMS = CHUNKS * PACK
+PLANE_STEP = 4
+FIRST_VECTOR_SUM = TILES - PACK
+WARM_PASSES = 4
 
-SMALLEST_DEG = 2.0**-100
+BIG = 2.0**60
+
+VISITS = (
+    [(g, 0, 4) for g in range(4)]
+    + [(g, 4, 6) for g in range(4)]
+    + [(g, 0, 6) for g in range(4, 7)]
+    + [(g, 6, 8) for g in range(7)]
+    + [(7, 0, 8)]
+)
 
 FLOPS = 2 * NODES * NODES * FEATS + 2 * NODES * FEATS * FEATS
+
+
+def passes_in_step(s):
+    if s < 18:
+        return 0
+    if s < 26:
+        return 8
+    return 16 if s < 28 else 18
 
 
 def tile_gcnlayer_pb_t_kernel(tc, h_ln, adj, W2, b2, out):
     nc = tc.nc
 
     adj_tiles = adj.rearrange("(g p e) j -> p g e j", p=P, e=PACK)
-    h_ln_spans = h_ln.rearrange("(g p e) k -> p g (e k)", p=P, e=PACK)
-    out_spans = out.rearrange("(g p e) f -> p g (e f)", p=P, e=PACK)
+    h_ln_groups = h_ln.rearrange("(g p e) k -> p g (e k)", p=P, e=PACK)
+    out_groups = out.rearrange("(g p e) f -> p g (e f)", p=P, e=PACK)
 
-    with tc.tile_pool(name="keep", bufs=1) as keep, tc.psum_pool(name="psum", bufs=8) as psum:
+    with tc.tile_pool(name="keep", bufs=1) as keep, tc.tile_pool(name="stream", bufs=2) as stream, tc.psum_pool(
+        name="psum", bufs=1
+    ) as psum:
         ident_f32 = keep.tile([P, P], F32)
         make_identity(nc, ident_f32[:])
         ident_bf16 = keep.tile([P, P], BF16)
         make_identity(nc, ident_bf16[:])
         w2_sb = keep.tile([FEATS, FEATS], BF16)
         nc.scalar.dma_start(out=w2_sb[:], in_=W2)
-        ones = keep.tile([P, P], BF16)
-        nc.vector.memset(ones[:], 1.0)
         bias_rows = keep.tile([P, FEATS], BF16)
         nc.vector.memset(bias_rows[:], 0.0)
         nc.scalar.dma_start(out=bias_rows[0:1, :], in_=b2.rearrange("(o f) -> o f", o=1))
+        warm_values = keep.tile([P, P * PACK], BF16, align_bytes=64)
+        nc.vector.memset(warm_values[:], 1.0)
+        ones = warm_values[:, 0:P]
+        one_column = keep.tile([P, 1], F32)
+        nc.vector.memset(one_column[:], 1.0)
+        warm_codes = keep.tile([P, P], U32, align_bytes=64)
+        warm_scales = keep.tile([P, P], U8, align_bytes=64)
+        nc.vector.quantize_mx(out=warm_codes[:].bitcast(FP8X4), scales=warm_scales[:], in_=warm_values[:])
         fold = keep.tile([P, CHUNKS, P], F32)
         nc.vector.memset(fold[:], 0.0)
         for chunk in range(CHUNKS):
@@ -62,172 +87,307 @@ def tile_gcnlayer_pb_t_kernel(tc, h_ln, adj, W2, b2, out):
                 op=ALU.add,
             )
         table_warmer = keep.tile([P, 1], F32)
-        nc.vector.memset(table_warmer[:], 1.0)
-        nc.scalar.activation(out=table_warmer[:], in_=table_warmer[:], func=ACT.Sqrt)
+        nc.scalar.activation(out=table_warmer[:], in_=one_column[:], func=ACT.Abs_reciprocal_sqrt)
 
         adj_codes = keep.tile([P, TILES, PASSES * P], U32, align_bytes=64)
-        adj_scales = keep.tile([P, TILES, PASSES * P], U8, align_bytes=64)
-        h_lnT = keep.tile([FEATS, NODES], BF16)
-        sums_tensor = psum.tile([P, CHUNKS * TILES], F32, tag="bank")
+        adj_planes = keep.tile([P, GROUPS, PASSES * P], U8, align_bytes=64)
+        hs_codes = keep.tile([P, PASSES * FEATS], U32, align_bytes=64)
+        hs_scales = keep.tile([P, PASSES * FEATS], U8, align_bytes=64)
+        acc = keep.tile([P, GROUPS, PACK * FEATS], F32)
+        dinv = keep.tile([P, TILES], F32)
+        vector_sums = keep.tile([P, HALVES, PACK], F32)
+        sums = psum.tile([P, BANK], F32, tag="sums")
+        first_folded = GROUPS * SUMS
 
-        with tc.tile_pool(name="stream", bufs=1) as stream:
-            turned = {}
-            for s in range(TILES + 1):
-                if s < TILES:
-                    rows = stream.tile([P, NODES], BF16, tag="rows", bufs=3)
-                    nc.sync.dma_start(out=rows[:], in_=adj_tiles[:, s // PACK, s % PACK, :])
+        rows_of = {}
+        paired_of = {}
+        grouped_of = {}
+        features_of = {}
+        h_lnT_of = {}
+        h_of = {}
+        work = {"next": 0, "bank": None, "ready": []}
+        jobs = [(v, t, c) for v, (g, lo, hi) in enumerate(VISITS) for t in range(PACK) for c in range(lo, hi)]
 
-                    paired = stream.tile([P, HALVES, 2, WORDS_IN_HALF // 2], F32, tag="paired", bufs=2)
-                    for half in range(HALVES):
-                        first_word = half * WORDS_IN_HALF
-                        nc.vector.tensor_copy(
-                            out=paired[:, half, :, :],
-                            in_=rows[:]
-                            .bitcast(F32)[:, first_word : first_word + WORDS_IN_HALF]
-                            .rearrange("p (n u) -> p u n", u=2),
-                        )
+        def load(s):
+            rows = stream.tile([P, NODES], BF16, tag="rows", bufs=3)
+            pieces = 4 if s == 0 else 1
+            width = NODES // pieces
+            for i in range(pieces):
+                nc.sync.dma_start(
+                    out=rows[:, i * width : (i + 1) * width],
+                    in_=adj_tiles[:, s // PACK, s % PACK, i * width : (i + 1) * width],
+                )
+            rows_of[s] = rows
 
-                    place = s % FEATURE_GROUP
-                    if place == 0:
-                        features = stream.tile([P, FEATURE_GROUP * FEATS], BF16, tag="features", bufs=2)
-                        first_span = s // PACK
-                        nc.sync.dma_start(
-                            out=features[:].rearrange("p (g x) -> p g x", x=PACK * FEATS),
-                            in_=h_ln_spans[:, first_span : first_span + FEATURE_GROUP // PACK, :],
-                        )
-                        features_bank = psum.tile([FEATS, FEATURE_GROUP * P], BF16, tag="bank")
+        def load_features(g):
+            features = stream.tile([P, PACK * FEATS], BF16, tag="features")
+            nc.sync.dma_start(out=features[:], in_=h_ln_groups[:, g, :])
+            features_of[g] = features
+
+        def sort(s, half):
+            paired = stream.tile([P, HALF], BF16, tag="paired", bufs=4)
+            source = rows_of[s][:, half * HALF : (half + 1) * HALF]
+            if s < FIRST_VECTOR_SUM:
+                nc.vector.tensor_copy(
+                    out=paired[:].bitcast(F32).rearrange("p (u n) -> p u n", u=2),
+                    in_=source.bitcast(F32).rearrange("p (n u) -> p u n", u=2),
+                )
+            else:
+                nc.vector.tensor_scalar(
+                    out=paired[:].rearrange("p (u n e) -> p u n e", u=2, e=2),
+                    in0=source.rearrange("p (n u e) -> p u n e", u=2, e=2),
+                    scalar1=1.0,
+                    scalar2=None,
+                    op0=ALU.mult,
+                    op1=ALU.add,
+                    accum_out=vector_sums[:, half, s % PACK : s % PACK + 1],
+                )
+            paired_of[s, half] = paired
+
+        def turn(s, half):
+            words = paired_of[s, half][:].bitcast(F32).rearrange("p (u n) -> p u n", u=2)
+            grouped = stream.tile([P, HALF], BF16, tag="grouped", bufs=5, align_bytes=64)
+            grouped_words = grouped[:].bitcast(F32).rearrange("q (c i u) -> q c i u", i=P, u=2)
+            for b in range(BANKS_IN_HALF):
+                first = b * PASSES_IN_BANK
+                bank = psum.tile([P, BANK], F32, tag="turn", bufs=4)
+                for place in range(2 * PASSES_IN_BANK):
+                    c, u = first + place // 2, place % 2
                     nc.tensor.transpose(
-                        features_bank[:, place * P : (place + 1) * P],
-                        features[:, place * FEATS : (place + 1) * FEATS],
-                        ident_bf16[:],
+                        bank[:, place * P : (place + 1) * P],
+                        words[:, u, c * P : (c + 1) * P],
+                        ident_f32[:],
                     )
-                    if place == FEATURE_GROUP - 1:
-                        nc.scalar.copy(
-                            out=h_lnT[:, (s - place) * P : (s + 1) * P], in_=features_bank[:]
-                        )
+                nc.scalar.copy(
+                    out=grouped_words[:, first : first + PASSES_IN_BANK, :, :],
+                    in_=bank[:].rearrange("q (c u i) -> q c i u", c=PASSES_IN_BANK, u=2),
+                )
+            grouped_of[s, half] = grouped
 
-                    grouped = stream.tile([P, NODES], BF16, tag="grouped", bufs=2, align_bytes=64)
-                    grouped_words = grouped[:].bitcast(F32).rearrange(
-                        "q (c i u) -> q c i u", c=PASSES, u=2
-                    )
-                    for b in range(BANKS_IN_TILE):
-                        bank = psum.tile([P, BANK], F32, tag="bank")
-                        for place in range(2 * PASSES_IN_BANK):
-                            c, u = b * PASSES_IN_BANK + place // 2, place % 2
-                            half, c_in_half = c // PASSES_IN_HALF, c % PASSES_IN_HALF
-                            nc.tensor.transpose(
-                                bank[:, place * P : (place + 1) * P],
-                                paired[:, half, u, c_in_half * P : (c_in_half + 1) * P],
-                                ident_f32[:],
-                            )
-                        nc.scalar.copy(
-                            out=grouped_words[:, b * PASSES_IN_BANK : (b + 1) * PASSES_IN_BANK, :, :],
-                            in_=bank[:].rearrange("q (c u i) -> q c i u", c=PASSES_IN_BANK, u=2),
-                        )
-                    turned[s] = grouped
-                if s >= 1:
-                    for chunk in range(CHUNKS):
-                        for c in range(PASSES):
-                            first_col = (c * P + chunk * ROWS_IN_CHUNK) * PACK
-                            nc.tensor.matmul(
-                                sums_tensor[:, chunk * TILES + s - 1 : chunk * TILES + s],
-                                lhsT=turned[s - 1][:, first_col : first_col + P],
-                                rhs=ones[:, 0:1],
-                                start=(c == 0),
-                                stop=(c == PASSES - 1),
-                            )
-                    nc.vector.quantize_mx(
-                        out=adj_codes[:, s - 1, :].bitcast(FP8X4),
-                        scales=adj_scales[:, s - 1, :],
-                        in_=turned[s - 1][:],
+        def quantise(s, half):
+            cols = slice(half * PASSES_IN_HALF * P, (half + 1) * PASSES_IN_HALF * P)
+            nc.vector.quantize_mx(
+                out=adj_codes[:, s, cols].bitcast(FP8X4),
+                scales=adj_planes[PLANE_STEP * (s % PACK) : P, s // PACK, cols],
+                in_=grouped_of[s, half][:],
+            )
+
+        def sum_rows(s, chunks):
+            for chunk in chunks:
+                col = (s // PACK) * SUMS + chunk * PACK + s % PACK
+                for c in range(PASSES):
+                    first_col = ((c % PASSES_IN_HALF) * P + chunk * ROWS_IN_CHUNK) * PACK
+                    nc.tensor.matmul(
+                        sums[:, col : col + 1],
+                        lhsT=grouped_of[s, c // PASSES_IN_HALF][:, first_col : first_col + P],
+                        rhs=ones[:, 0:1],
+                        start=(c == 0),
+                        stop=(c == PASSES - 1),
                     )
 
-        with tc.tile_pool(name="tail", bufs=1) as tail:
-            sums_by_value = tail.tile([P, CHUNKS * TILES], F32)
-            nc.vector.tensor_copy(out=sums_by_value[:], in_=sums_tensor[:])
-            folded_bank = psum.tile([P, BANK], F32, tag="bank")
-            folded = folded_bank[:, :TILES]
+        def copy_sums(g):
+            sums_sb = stream.tile([P, SUMS], F32, tag="sums_sb")
+            nc.scalar.copy(out=sums_sb[:], in_=sums[:, g * SUMS : (g + 1) * SUMS])
+            return sums_sb
+
+        def fold_sums(g, sums_sb):
             for chunk in range(CHUNKS):
                 nc.tensor.matmul(
-                    folded,
+                    sums[:, first_folded + g * PACK : first_folded + (g + 1) * PACK],
                     lhsT=fold[:, chunk, :],
-                    rhs=sums_by_value[:, chunk * TILES : (chunk + 1) * TILES],
+                    rhs=sums_sb[:, chunk * PACK : (chunk + 1) * PACK],
                     start=(chunk == 0),
                     stop=(chunk == CHUNKS - 1),
                 )
-            deg = tail.tile([P, TILES], F32)
-            nc.vector.tensor_scalar_add(out=deg[:], in0=folded, scalar1=1.0)
-            root = tail.tile([P, TILES], F32)
-            nc.vector.tensor_scalar_max(out=root[:], in0=deg[:], scalar1=SMALLEST_DEG)
-            nc.scalar.activation(out=root[:], in_=root[:], func=ACT.Sqrt)
-            one_over_root = tail.tile([P, TILES], F32)
-            nc.vector.reciprocal(out=one_over_root[:], in_=root[:])
-            dinv = tail.tile([P, TILES], F32)
+
+        def row_sums_of(g):
+            if g < GROUPS - 1:
+                return sums[:, first_folded + g * PACK : first_folded + (g + 1) * PACK]
+            total = stream.tile([P, PACK], F32, tag="total")
+            nc.vector.tensor_add(out=total[:], in0=vector_sums[:, 0, :], in1=vector_sums[:, 1, :])
+            return total[:]
+
+        def reciprocal_root(row_sums):
+            root = stream.tile([P, PACK], F32, tag="root")
+            nc.scalar.activation(
+                out=root[:], in_=row_sums, func=ACT.Abs_reciprocal_sqrt, bias=one_column[:]
+            )
+            return root
+
+        def make_dinv(g, row_sums, root):
+            positive = stream.tile([P, PACK], F32, tag="positive")
+            nc.vector.tensor_scalar(
+                out=positive[:], in0=row_sums, scalar1=-1.0, scalar2=None, op0=ALU.is_gt
+            )
             nc.vector.scalar_tensor_tensor(
-                out=dinv[:], in0=deg[:], scalar=0.0, in1=one_over_root[:], op0=ALU.is_gt, op1=ALU.mult
+                out=dinv[:, g * PACK : (g + 1) * PACK],
+                in0=root[:],
+                scalar=BIG,
+                in1=positive[:],
+                op0=ALU.min,
+                op1=ALU.mult,
             )
-            dinv_squared = tail.tile([P, TILES], F32)
-            nc.vector.tensor_mul(out=dinv_squared[:], in0=dinv[:], in1=dinv[:])
 
-            hs_grouped = tail.tile([P, PASSES, FEATS * PACK], BF16, align_bytes=64)
-            self_term = tail.tile([P, TILES * FEATS], F32)
-            for c in range(PASSES):
-                h_bank = psum.tile([P, BANK], F32, tag="bank")
-                for t in range(PACK):
-                    s = PACK * c + t
-                    h_tile = h_bank[:, t * FEATS : (t + 1) * FEATS]
-                    nc.tensor.matmul(h_tile, lhsT=ones[:], rhs=bias_rows[:], start=True, stop=False)
-                    nc.tensor.matmul(
-                        h_tile, lhsT=h_lnT[:, s * P : (s + 1) * P], rhs=w2_sb[:], start=False, stop=True
-                    )
-                nc.vector.tensor_tensor(
-                    out=hs_grouped[:, c, :].rearrange("q (f t) -> q f t", t=PACK),
-                    in0=h_bank[:].rearrange("q (t f) -> q f t", t=PACK),
-                    in1=dinv[:, PACK * c : PACK * (c + 1)].unsqueeze(1).to_broadcast([P, FEATS, PACK]),
-                    op=ALU.mult,
+        def turn_features(g):
+            bank = psum.tile([P, PACK * P], BF16, tag="h")
+            for t in range(PACK):
+                nc.tensor.transpose(
+                    bank[:, t * P : (t + 1) * P], features_of[g][:, t * FEATS : (t + 1) * FEATS], ident_bf16[:]
                 )
-                for t in range(PACK):
-                    s = PACK * c + t
-                    nc.scalar.activation(
-                        out=self_term[:, s * FEATS : (s + 1) * FEATS],
-                        in_=h_bank[:, t * FEATS : (t + 1) * FEATS],
-                        func=ACT.Copy,
-                        scale=dinv_squared[:, s : s + 1],
-                    )
-            hs_codes = tail.tile([P, PASSES * FEATS], U32, align_bytes=64)
-            hs_scales = tail.tile([P, PASSES * FEATS], U8, align_bytes=64)
+            h_lnT_of[g] = bank
+
+        def copy_features(g):
+            h_lnT = stream.tile([P, PACK * P], BF16, tag="h_lnT")
+            nc.scalar.copy(out=h_lnT[:], in_=h_lnT_of[g][:])
+            h_lnT_of[g] = h_lnT
+
+        def make_h(g):
+            h = psum.tile([P, PACK * FEATS], F32, tag="h")
+            for t in range(PACK):
+                h_tile = h[:, t * FEATS : (t + 1) * FEATS]
+                nc.tensor.matmul(h_tile, lhsT=ones, rhs=bias_rows[:], start=True, stop=False)
+                nc.tensor.matmul(
+                    h_tile, lhsT=h_lnT_of[g][:, t * P : (t + 1) * P], rhs=w2_sb[:], start=False, stop=True
+                )
+            h_of[g] = h
+
+        def group_hs(g):
+            hs_grouped = stream.tile([P, FEATS * PACK], BF16, tag="hs_grouped", align_bytes=64)
+            nc.vector.tensor_tensor(
+                out=hs_grouped[:].rearrange("q (f t) -> q f t", t=PACK),
+                in0=h_of[g][:].rearrange("q (t f) -> q f t", t=PACK),
+                in1=dinv[:, PACK * g : PACK * (g + 1)].unsqueeze(1).to_broadcast([P, FEATS, PACK]),
+                op=ALU.mult,
+            )
+            return hs_grouped
+
+        def quantise_hs(g, hs_grouped):
             nc.vector.quantize_mx(
-                out=hs_codes[:].bitcast(FP8X4),
-                scales=hs_scales[:],
-                in_=hs_grouped[:].rearrange("q c x -> q (c x)"),
+                out=hs_codes[:, g * FEATS : (g + 1) * FEATS].bitcast(FP8X4),
+                scales=hs_scales[:, g * FEATS : (g + 1) * FEATS],
+                in_=hs_grouped[:],
             )
 
-            for first in range(0, TILES, TILES_IN_BANK):
-                agg_bank = psum.tile([P, BANK], F32, tag="bank")
-                for place in range(TILES_IN_BANK):
-                    s = first + place
-                    for c in range(PASSES):
-                        nc.tensor.matmul_mx(
-                            out=agg_bank[:, place * FEATS : (place + 1) * FEATS],
-                            lhsT=adj_codes[:, s, c * P : (c + 1) * P].bitcast(FP8X4),
-                            lhsT_scale=adj_scales[:, s, c * P : (c + 1) * P],
-                            rhs=hs_codes[:, c * FEATS : (c + 1) * FEATS].bitcast(FP8X4),
-                            rhs_scale=hs_scales[:, c * FEATS : (c + 1) * FEATS],
-                            start=(c == 0),
-                            stop=(c == PASSES - 1),
-                        )
-                result = tail.tile([P, BANK], F32, tag="result", bufs=3)
-                for place in range(TILES_IN_BANK):
-                    s = first + place
-                    nc.vector.scalar_tensor_tensor(
-                        out=result[:, place * FEATS : (place + 1) * FEATS],
-                        in0=agg_bank[:, place * FEATS : (place + 1) * FEATS],
-                        scalar=dinv[:, s : s + 1],
-                        in1=self_term[:, s * FEATS : (s + 1) * FEATS],
-                        op0=ALU.mult,
-                        op1=ALU.add,
-                    )
-                nc.sync.dma_start(
-                    out=out_spans[:, first // PACK, :],
-                    in_=result[:],
+        def keep_hs(g):
+            for t in range(PACK):
+                s = PACK * g + t
+                nc.scalar.activation(
+                    out=acc[:, g, t * FEATS : (t + 1) * FEATS],
+                    in_=h_of[g][:, t * FEATS : (t + 1) * FEATS],
+                    func=ACT.Copy,
+                    scale=dinv[:, s : s + 1],
                 )
+
+        def warm(count):
+            bank = psum.tile([P, BANK], F32, tag="agg", bufs=2)
+            for i in range(count):
+                nc.tensor.matmul_mx(
+                    out=bank[:, 0:P],
+                    lhsT=warm_codes[:].bitcast(FP8X4),
+                    lhsT_scale=warm_scales[:],
+                    rhs=warm_codes[:].bitcast(FP8X4),
+                    rhs_scale=warm_scales[:],
+                    start=True,
+                    stop=True,
+                )
+
+        def multiply(count):
+            for v, t, c in jobs[work["next"] : work["next"] + count]:
+                g, lo, hi = VISITS[v]
+                if t == 0 and c == lo:
+                    work["bank"] = psum.tile([P, BANK], F32, tag="agg", bufs=2, name="agg")
+                s = PACK * g + t
+                nc.tensor.matmul_mx(
+                    out=work["bank"][:, t * FEATS : (t + 1) * FEATS],
+                    lhsT=adj_codes[:, s, c * P : (c + 1) * P].bitcast(FP8X4),
+                    lhsT_scale=adj_planes[PLANE_STEP * t : P, g, c * P : (c + 1) * P],
+                    rhs=hs_codes[:, c * FEATS : (c + 1) * FEATS].bitcast(FP8X4),
+                    rhs_scale=hs_scales[:, c * FEATS : (c + 1) * FEATS],
+                    start=(c == lo),
+                    stop=(c == hi - 1),
+                )
+                if t == PACK - 1 and c == hi - 1:
+                    work["ready"].append((g, hi, work["bank"]))
+            work["next"] += count
+
+        def collect(visits):
+            for g, hi, bank in visits:
+                nc.vector.tensor_add(out=acc[:, g, :], in0=bank[:], in1=acc[:, g, :])
+                if hi == PASSES:
+                    for t in range(PACK):
+                        s = PACK * g + t
+                        nc.scalar.activation(
+                            out=acc[:, g, t * FEATS : (t + 1) * FEATS],
+                            in_=acc[:, g, t * FEATS : (t + 1) * FEATS],
+                            func=ACT.Copy,
+                            scale=dinv[:, s : s + 1],
+                        )
+                    nc.sync.dma_start(out=out_groups[:, g, :], in_=acc[:, g, :])
+
+        with tc.manual_schedule():
+            load(0)
+            load(1)
+            load(2)
+            warm(8)
+            for half in range(HALVES):
+                sort(0, half)
+            folding = None
+            grouping = None
+            for s in range(TILES):
+                turning = [g for g in range(GROUPS) if s == min(PACK * g + 3, TILES - 2)]
+                making = [g for g in range(GROUPS) if s == min(PACK * g + 4, TILES - 1)]
+                scaling = [g for g in range(GROUPS) if s == min(PACK * g + 5, TILES - 1)]
+                finishing = [g for g in range(GROUPS) if s == PACK * g + 6]
+                if s + 3 < TILES:
+                    load(s + 3)
+                if s % PACK == 0:
+                    load_features(s // PACK)
+
+                if s + 1 < TILES:
+                    sort(s + 1, 0)
+                for g in finishing:
+                    quantise_hs(g, grouping)
+                for g in making:
+                    copy_features(g)
+                turn(s, 0)
+                if s >= 1:
+                    quantise(s - 1, 0)
+                    if s - 1 < FIRST_VECTOR_SUM:
+                        sum_rows(s - 1, [0, 1])
+                for g in finishing:
+                    keep_hs(g)
+                for g in scaling:
+                    if g < GROUPS - 1:
+                        fold_sums(g, folding)
+                    row_sums = row_sums_of(g)
+                    root = reciprocal_root(row_sums)
+                if s + 1 < TILES:
+                    sort(s + 1, 1)
+                turn(s, 1)
+                if s >= 1:
+                    quantise(s - 1, 1)
+                    if s - 1 < FIRST_VECTOR_SUM:
+                        sum_rows(s - 1, [2, 3])
+                        if s % PACK == 0:
+                            folding = copy_sums(s // PACK - 1)
+                for g in turning:
+                    turn_features(g)
+                for g in making:
+                    make_h(g)
+                for g in scaling:
+                    make_dinv(g, row_sums, root)
+                    grouping = group_hs(g)
+                collect(work["ready"])
+                work["ready"] = []
+                if passes_in_step(s) == 0:
+                    warm(WARM_PASSES)
+                multiply(passes_in_step(s))
+
+            quantise_hs(GROUPS - 1, grouping)
+            keep_hs(GROUPS - 1)
+            for half in range(HALVES):
+                quantise(TILES - 1, half)
+            for v in range(jobs[work["next"]][0], len(VISITS)):
+                multiply(len([1 for job in jobs[work["next"] :] if job[0] == v]))
+                collect(work["ready"])
+                work["ready"] = []

@@ -27,7 +27,7 @@ CHUNKS = P // ROWS_IN_CHUNK
 SUMS = CHUNKS * PACK
 PLANE_STEP = 4
 FIRST_VECTOR_SUM = TILES - PACK
-WARM_PASSES = 4
+WARM_PASSES = 8
 
 BIG = 2.0**60
 
@@ -43,11 +43,11 @@ FLOPS = 2 * NODES * NODES * FEATS + 2 * NODES * FEATS * FEATS
 
 
 def passes_in_step(s):
-    if s < 18:
+    if s < 19:
         return 0
-    if s < 26:
+    if s < 27:
         return 8
-    return 16 if s < 28 else 18
+    return 16 if s < 29 else 24
 
 
 def tile_gcnlayer_pb_t_kernel(tc, h_ln, adj, W2, b2, out):
@@ -119,10 +119,10 @@ def tile_gcnlayer_pb_t_kernel(tc, h_ln, adj, W2, b2, out):
                 )
             rows_of[s] = rows
 
-        def load_features(g):
-            features = stream.tile([P, PACK * FEATS], BF16, tag="features")
-            nc.sync.dma_start(out=features[:], in_=h_ln_groups[:, g, :])
-            features_of[g] = features
+        def load_features(pair):
+            features = stream.tile([P, 2, PACK * FEATS], BF16, tag="features", bufs=1)
+            nc.sync.dma_start(out=features[:], in_=h_ln_groups[:, 2 * pair : 2 * pair + 2, :])
+            features_of[pair] = features
 
         def sort(s, half):
             paired = stream.tile([P, HALF], BF16, tag="paired", bufs=4)
@@ -212,12 +212,14 @@ def tile_gcnlayer_pb_t_kernel(tc, h_ln, adj, W2, b2, out):
             nc.scalar.activation(
                 out=root[:], in_=row_sums, func=ACT.Abs_reciprocal_sqrt, bias=one_column[:]
             )
-            return root
+            sums_sb = stream.tile([P, PACK], F32, tag="folded_sb")
+            nc.scalar.copy(out=sums_sb[:], in_=row_sums)
+            return root, sums_sb
 
-        def make_dinv(g, row_sums, root):
+        def make_dinv(g, root, row_sums):
             positive = stream.tile([P, PACK], F32, tag="positive")
             nc.vector.tensor_scalar(
-                out=positive[:], in0=row_sums, scalar1=-1.0, scalar2=None, op0=ALU.is_gt
+                out=positive[:], in0=row_sums[:], scalar1=-1.0, scalar2=None, op0=ALU.is_gt
             )
             nc.vector.scalar_tensor_tensor(
                 out=dinv[:, g * PACK : (g + 1) * PACK],
@@ -228,18 +230,21 @@ def tile_gcnlayer_pb_t_kernel(tc, h_ln, adj, W2, b2, out):
                 op1=ALU.mult,
             )
 
-        def turn_features(g):
-            bank = psum.tile([P, PACK * P], BF16, tag="h")
-            for t in range(PACK):
-                nc.tensor.transpose(
-                    bank[:, t * P : (t + 1) * P], features_of[g][:, t * FEATS : (t + 1) * FEATS], ident_bf16[:]
-                )
-            h_lnT_of[g] = bank
+        def turn_features(pair):
+            bank = psum.tile([P, 2, PACK * P], BF16, tag="h")
+            for i in range(2):
+                for t in range(PACK):
+                    nc.tensor.transpose(
+                        bank[:, i, t * P : (t + 1) * P],
+                        features_of[pair][:, i, t * FEATS : (t + 1) * FEATS],
+                        ident_bf16[:],
+                    )
+            h_lnT_of[pair] = bank
 
-        def copy_features(g):
-            h_lnT = stream.tile([P, PACK * P], BF16, tag="h_lnT")
-            nc.scalar.copy(out=h_lnT[:], in_=h_lnT_of[g][:])
-            h_lnT_of[g] = h_lnT
+        def copy_features(pair):
+            h_lnT = stream.tile([P, 2, PACK * P], BF16, tag="h_lnT", bufs=1)
+            nc.scalar.copy(out=h_lnT[:], in_=h_lnT_of[pair][:])
+            h_lnT_of[pair] = h_lnT
 
         def make_h(g):
             h = psum.tile([P, PACK * FEATS], F32, tag="h")
@@ -247,7 +252,7 @@ def tile_gcnlayer_pb_t_kernel(tc, h_ln, adj, W2, b2, out):
                 h_tile = h[:, t * FEATS : (t + 1) * FEATS]
                 nc.tensor.matmul(h_tile, lhsT=ones, rhs=bias_rows[:], start=True, stop=False)
                 nc.tensor.matmul(
-                    h_tile, lhsT=h_lnT_of[g][:, t * P : (t + 1) * P], rhs=w2_sb[:], start=False, stop=True
+                    h_tile, lhsT=h_lnT_of[g // 2][:, g % 2, t * P : (t + 1) * P], rhs=w2_sb[:], start=False, stop=True
                 )
             h_of[g] = h
 
@@ -328,54 +333,53 @@ def tile_gcnlayer_pb_t_kernel(tc, h_ln, adj, W2, b2, out):
             load(0)
             load(1)
             load(2)
-            warm(8)
+            warm(24)
             for half in range(HALVES):
                 sort(0, half)
             folding = None
             grouping = None
+            roots = {}
             for s in range(TILES):
-                turning = [g for g in range(GROUPS) if s == min(PACK * g + 3, TILES - 2)]
-                making = [g for g in range(GROUPS) if s == min(PACK * g + 4, TILES - 1)]
-                scaling = [g for g in range(GROUPS) if s == min(PACK * g + 5, TILES - 1)]
-                finishing = [g for g in range(GROUPS) if s == PACK * g + 6]
+                last = [GROUPS - 1]
+                making = last if s == TILES - 1 else [g for g in range(GROUPS - 1) if s == PACK * g + 4]
+                folding_now = last if s == TILES - 1 else [g for g in range(GROUPS - 1) if s == PACK * g + 5]
+                scaling = last if s == TILES - 1 else [g for g in range(GROUPS - 1) if s == PACK * g + 6]
+                finishing = [g for g in range(GROUPS - 1) if s == PACK * g + 7]
                 if s + 3 < TILES:
                     load(s + 3)
-                if s % PACK == 0:
-                    load_features(s // PACK)
+                if s % 8 == 0:
+                    load_features(s // 8)
 
                 if s + 1 < TILES:
                     sort(s + 1, 0)
                 for g in finishing:
                     quantise_hs(g, grouping)
-                for g in making:
-                    copy_features(g)
+                if s % 8 == 4:
+                    copy_features(s // 8)
                 turn(s, 0)
                 if s >= 1:
                     quantise(s - 1, 0)
-                    if s - 1 < FIRST_VECTOR_SUM:
-                        sum_rows(s - 1, [0, 1])
-                for g in finishing:
-                    keep_hs(g)
-                for g in scaling:
-                    if g < GROUPS - 1:
-                        fold_sums(g, folding)
-                    row_sums = row_sums_of(g)
-                    root = reciprocal_root(row_sums)
                 if s + 1 < TILES:
                     sort(s + 1, 1)
+                for g in finishing:
+                    keep_hs(g)
                 turn(s, 1)
                 if s >= 1:
                     quantise(s - 1, 1)
                     if s - 1 < FIRST_VECTOR_SUM:
-                        sum_rows(s - 1, [2, 3])
+                        sum_rows(s - 1, range(CHUNKS))
                         if s % PACK == 0:
                             folding = copy_sums(s // PACK - 1)
-                for g in turning:
-                    turn_features(g)
+                for g in folding_now:
+                    if g < GROUPS - 1:
+                        fold_sums(g, folding)
+                    roots[g] = reciprocal_root(row_sums_of(g))
+                if s % 8 == 3:
+                    turn_features(s // 8)
                 for g in making:
                     make_h(g)
                 for g in scaling:
-                    make_dinv(g, row_sums, root)
+                    make_dinv(g, *roots[g])
                     grouping = group_hs(g)
                 collect(work["ready"])
                 work["ready"] = []

@@ -25,9 +25,9 @@ BANKS_IN_HALF = PASSES_IN_HALF // PASSES_IN_BANK
 ROWS_IN_CHUNK = P // PACK
 CHUNKS = P // ROWS_IN_CHUNK
 SUMS = CHUNKS * PACK
+SUM_COLS = 8
 PLANE_STEP = 4
 FIRST_VECTOR_SUM = TILES - PACK
-WARM_PASSES = 8
 
 BIG = 2.0**60
 
@@ -95,9 +95,10 @@ def tile_gcnlayer_pb_t_kernel(tc, h_ln, adj, W2, b2, out):
         hs_scales = keep.tile([P, PASSES * FEATS], U8, align_bytes=64)
         acc = keep.tile([P, GROUPS, PACK * FEATS], F32)
         dinv = keep.tile([P, TILES], F32)
-        vector_sums = keep.tile([P, HALVES, PACK], F32)
+        vector_sums = keep.tile([P, HALVES, TILES], F32)
         sums = psum.tile([P, BANK], F32, tag="sums")
-        first_folded = GROUPS * SUMS
+        first_folded = 2 * SUMS * SUM_COLS
+        part_sums = sums[:, :first_folded].rearrange("p (g k e) -> p g k e", g=2, e=SUM_COLS)
 
         rows_of = {}
         paired_of = {}
@@ -127,7 +128,7 @@ def tile_gcnlayer_pb_t_kernel(tc, h_ln, adj, W2, b2, out):
         def sort(s, half):
             paired = stream.tile([P, HALF], BF16, tag="paired", bufs=4)
             source = rows_of[s][:, half * HALF : (half + 1) * HALF]
-            if s < FIRST_VECTOR_SUM:
+            if half == 0 and s < FIRST_VECTOR_SUM:
                 nc.vector.tensor_copy(
                     out=paired[:].bitcast(F32).rearrange("p (u n) -> p u n", u=2),
                     in_=source.bitcast(F32).rearrange("p (n u) -> p u n", u=2),
@@ -140,7 +141,7 @@ def tile_gcnlayer_pb_t_kernel(tc, h_ln, adj, W2, b2, out):
                     scalar2=None,
                     op0=ALU.mult,
                     op1=ALU.add,
-                    accum_out=vector_sums[:, half, s % PACK : s % PACK + 1],
+                    accum_out=vector_sums[:, half, s : s + 1],
                 )
             paired_of[s, half] = paired
 
@@ -172,22 +173,21 @@ def tile_gcnlayer_pb_t_kernel(tc, h_ln, adj, W2, b2, out):
                 in_=grouped_of[s, half][:],
             )
 
-        def sum_rows(s, chunks):
-            for chunk in chunks:
-                col = (s // PACK) * SUMS + chunk * PACK + s % PACK
-                for c in range(PASSES):
-                    first_col = ((c % PASSES_IN_HALF) * P + chunk * ROWS_IN_CHUNK) * PACK
+        def sum_rows(s):
+            for chunk in range(CHUNKS):
+                for c in range(PASSES_IN_HALF):
+                    first_col = (c * P + chunk * ROWS_IN_CHUNK) * PACK
                     nc.tensor.matmul(
-                        sums[:, col : col + 1],
-                        lhsT=grouped_of[s, c // PASSES_IN_HALF][:, first_col : first_col + P],
-                        rhs=ones[:, 0:1],
+                        part_sums[:, s // PACK % 2, chunk * PACK + s % PACK, :],
+                        lhsT=grouped_of[s, 0][:, first_col : first_col + P],
+                        rhs=ones[:, 0:SUM_COLS],
                         start=(c == 0),
-                        stop=(c == PASSES - 1),
+                        stop=(c == PASSES_IN_HALF - 1),
                     )
 
         def copy_sums(g):
             sums_sb = stream.tile([P, SUMS], F32, tag="sums_sb")
-            nc.scalar.copy(out=sums_sb[:], in_=sums[:, g * SUMS : (g + 1) * SUMS])
+            nc.scalar.copy(out=sums_sb[:], in_=part_sums[:, g % 2, :, 0])
             return sums_sb
 
         def fold_sums(g, sums_sb):
@@ -201,20 +201,21 @@ def tile_gcnlayer_pb_t_kernel(tc, h_ln, adj, W2, b2, out):
                 )
 
         def row_sums_of(g):
-            if g < GROUPS - 1:
-                return sums[:, first_folded + g * PACK : first_folded + (g + 1) * PACK]
             total = stream.tile([P, PACK], F32, tag="total")
-            nc.vector.tensor_add(out=total[:], in0=vector_sums[:, 0, :], in1=vector_sums[:, 1, :])
-            return total[:]
+            tiles = slice(g * PACK, (g + 1) * PACK)
+            if g < GROUPS - 1:
+                first_half = sums[:, first_folded + g * PACK : first_folded + (g + 1) * PACK]
+            else:
+                first_half = vector_sums[:, 0, tiles]
+            nc.vector.tensor_add(out=total[:], in0=first_half, in1=vector_sums[:, 1, tiles])
+            return total
 
         def reciprocal_root(row_sums):
             root = stream.tile([P, PACK], F32, tag="root")
             nc.scalar.activation(
-                out=root[:], in_=row_sums, func=ACT.Abs_reciprocal_sqrt, bias=one_column[:]
+                out=root[:], in_=row_sums[:], func=ACT.Abs_reciprocal_sqrt, bias=one_column[:]
             )
-            sums_sb = stream.tile([P, PACK], F32, tag="folded_sb")
-            nc.scalar.copy(out=sums_sb[:], in_=row_sums)
-            return root, sums_sb
+            return root
 
         def make_dinv(g, root, row_sums):
             positive = stream.tile([P, PACK], F32, tag="positive")
@@ -333,16 +334,15 @@ def tile_gcnlayer_pb_t_kernel(tc, h_ln, adj, W2, b2, out):
             load(0)
             load(1)
             load(2)
-            warm(24)
+            warm(16)
             for half in range(HALVES):
                 sort(0, half)
             folding = None
             grouping = None
-            roots = {}
             for s in range(TILES):
                 last = [GROUPS - 1]
                 making = last if s == TILES - 1 else [g for g in range(GROUPS - 1) if s == PACK * g + 4]
-                folding_now = last if s == TILES - 1 else [g for g in range(GROUPS - 1) if s == PACK * g + 5]
+                folding_now = [g for g in range(GROUPS - 1) if s == PACK * g + 5]
                 scaling = last if s == TILES - 1 else [g for g in range(GROUPS - 1) if s == PACK * g + 6]
                 finishing = [g for g in range(GROUPS - 1) if s == PACK * g + 7]
                 if s + 3 < TILES:
@@ -357,6 +357,9 @@ def tile_gcnlayer_pb_t_kernel(tc, h_ln, adj, W2, b2, out):
                 if s % 8 == 4:
                     copy_features(s // 8)
                 turn(s, 0)
+                for g in scaling:
+                    row_sums = row_sums_of(g)
+                    root = reciprocal_root(row_sums)
                 if s >= 1:
                     quantise(s - 1, 0)
                 if s + 1 < TILES:
@@ -367,24 +370,20 @@ def tile_gcnlayer_pb_t_kernel(tc, h_ln, adj, W2, b2, out):
                 if s >= 1:
                     quantise(s - 1, 1)
                     if s - 1 < FIRST_VECTOR_SUM:
-                        sum_rows(s - 1, range(CHUNKS))
+                        sum_rows(s - 1)
                         if s % PACK == 0:
                             folding = copy_sums(s // PACK - 1)
                 for g in folding_now:
-                    if g < GROUPS - 1:
-                        fold_sums(g, folding)
-                    roots[g] = reciprocal_root(row_sums_of(g))
+                    fold_sums(g, folding)
                 if s % 8 == 3:
                     turn_features(s // 8)
                 for g in making:
                     make_h(g)
                 for g in scaling:
-                    make_dinv(g, *roots[g])
+                    make_dinv(g, root, row_sums)
                     grouping = group_hs(g)
                 collect(work["ready"])
                 work["ready"] = []
-                if passes_in_step(s) == 0:
-                    warm(WARM_PASSES)
                 multiply(passes_in_step(s))
 
             quantise_hs(GROUPS - 1, grouping)

@@ -27,7 +27,7 @@ CHUNKS = P // ROWS_IN_CHUNK
 SUMS = CHUNKS * PACK
 SUM_COLS = 8
 PLANE_STEP = 4
-FIRST_VECTOR_SUM = TILES - PACK
+FIRST_VECTOR_SUM = TILES - 1
 
 BIG = 2.0**60
 
@@ -77,15 +77,17 @@ def tile_gcnlayer_pb_t_kernel(tc, h_ln, adj, W2, b2, out):
         warm_codes = keep.tile([P, P], U32, align_bytes=64)
         warm_scales = keep.tile([P, P], U8, align_bytes=64)
         nc.vector.quantize_mx(out=warm_codes[:].bitcast(FP8X4), scales=warm_scales[:], in_=warm_values[:])
-        fold = keep.tile([P, CHUNKS, P], F32)
-        nc.vector.memset(fold[:], 0.0)
+        fold = keep.tile([P, CHUNKS, ROWS_IN_CHUNK], F32)
+        own_chunk = keep.tile([P, CHUNKS, PACK], F32)
+        nc.gpsimd.memset(own_chunk[:], 0.0)
         for chunk in range(CHUNKS):
             nc.vector.tensor_reduce(
-                out=fold[:, chunk, chunk * ROWS_IN_CHUNK : (chunk + 1) * ROWS_IN_CHUNK],
+                out=fold[:, chunk, :],
                 in_=ident_f32[:].rearrange("k (i t) -> k i t", t=PACK),
                 axis=mybir.AxisListType.X,
                 op=ALU.add,
             )
+            nc.gpsimd.memset(own_chunk[chunk * ROWS_IN_CHUNK : (chunk + 1) * ROWS_IN_CHUNK, chunk, :], 1.0)
         table_warmer = keep.tile([P, 1], F32)
         nc.scalar.activation(out=table_warmer[:], in_=one_column[:], func=ACT.Abs_reciprocal_sqrt)
 
@@ -95,10 +97,12 @@ def tile_gcnlayer_pb_t_kernel(tc, h_ln, adj, W2, b2, out):
         hs_scales = keep.tile([P, PASSES * FEATS], U8, align_bytes=64)
         acc = keep.tile([P, GROUPS, PACK * FEATS], F32)
         dinv = keep.tile([P, TILES], F32)
-        vector_sums = keep.tile([P, HALVES, TILES], F32)
+        vector_sums = keep.tile([P, HALVES], F32)
         sums = psum.tile([P, BANK], F32, tag="sums")
+        bias = keep.tile([P, FEATS], F32)
         first_folded = 2 * SUMS * SUM_COLS
         part_sums = sums[:, :first_folded].rearrange("p (g k e) -> p g k e", g=2, e=SUM_COLS)
+        folded = sums[:, first_folded : first_folded + GROUPS * SUMS].rearrange("p (g k) -> p g k", g=GROUPS)
 
         rows_of = {}
         paired_of = {}
@@ -128,7 +132,7 @@ def tile_gcnlayer_pb_t_kernel(tc, h_ln, adj, W2, b2, out):
         def sort(s, half):
             paired = stream.tile([P, HALF], BF16, tag="paired", bufs=4)
             source = rows_of[s][:, half * HALF : (half + 1) * HALF]
-            if half == 0 and s < FIRST_VECTOR_SUM:
+            if s < FIRST_VECTOR_SUM:
                 nc.vector.tensor_copy(
                     out=paired[:].bitcast(F32).rearrange("p (u n) -> p u n", u=2),
                     in_=source.bitcast(F32).rearrange("p (n u) -> p u n", u=2),
@@ -141,7 +145,7 @@ def tile_gcnlayer_pb_t_kernel(tc, h_ln, adj, W2, b2, out):
                     scalar2=None,
                     op0=ALU.mult,
                     op1=ALU.add,
-                    accum_out=vector_sums[:, half, s : s + 1],
+                    accum_out=vector_sums[:, half : half + 1],
                 )
             paired_of[s, half] = paired
 
@@ -175,14 +179,14 @@ def tile_gcnlayer_pb_t_kernel(tc, h_ln, adj, W2, b2, out):
 
         def sum_rows(s):
             for chunk in range(CHUNKS):
-                for c in range(PASSES_IN_HALF):
-                    first_col = (c * P + chunk * ROWS_IN_CHUNK) * PACK
+                for c in range(PASSES):
+                    first_col = (c % PASSES_IN_HALF * P + chunk * ROWS_IN_CHUNK) * PACK
                     nc.tensor.matmul(
                         part_sums[:, s // PACK % 2, chunk * PACK + s % PACK, :],
-                        lhsT=grouped_of[s, 0][:, first_col : first_col + P],
+                        lhsT=grouped_of[s, c // PASSES_IN_HALF][:, first_col : first_col + P],
                         rhs=ones[:, 0:SUM_COLS],
                         start=(c == 0),
-                        stop=(c == PASSES_IN_HALF - 1),
+                        stop=(c == PASSES - 1),
                     )
 
         def copy_sums(g):
@@ -191,24 +195,34 @@ def tile_gcnlayer_pb_t_kernel(tc, h_ln, adj, W2, b2, out):
             return sums_sb
 
         def fold_sums(g, sums_sb):
-            for chunk in range(CHUNKS):
-                nc.tensor.matmul(
-                    sums[:, first_folded + g * PACK : first_folded + (g + 1) * PACK],
-                    lhsT=fold[:, chunk, :],
-                    rhs=sums_sb[:, chunk * PACK : (chunk + 1) * PACK],
-                    start=(chunk == 0),
-                    stop=(chunk == CHUNKS - 1),
-                )
+            nc.tensor.matmul(
+                folded[:, g, :],
+                lhsT=fold[:].rearrange("k c i -> k (c i)"),
+                rhs=sums_sb[:],
+                start=True,
+                stop=True,
+            )
 
-        def row_sums_of(g):
-            total = stream.tile([P, PACK], F32, tag="total")
-            tiles = slice(g * PACK, (g + 1) * PACK)
-            if g < GROUPS - 1:
-                first_half = sums[:, first_folded + g * PACK : first_folded + (g + 1) * PACK]
-            else:
-                first_half = vector_sums[:, 0, tiles]
-            nc.vector.tensor_add(out=total[:], in0=first_half, in1=vector_sums[:, 1, tiles])
-            return total
+        def pick_own(g):
+            own = stream.tile([P, CHUNKS, PACK], F32, tag="own")
+            nc.vector.tensor_mul(
+                out=own[:], in0=folded[:, g, :].rearrange("p (c t) -> p c t", c=CHUNKS), in1=own_chunk[:]
+            )
+            return own
+
+        def add_own(g, own):
+            row_sums = stream.tile([P, PACK], F32, tag="row_sums")
+            nc.vector.tensor_reduce(
+                out=row_sums[:],
+                in_=own[:].rearrange("p c t -> p t c"),
+                axis=mybir.AxisListType.X,
+                op=ALU.add,
+            )
+            if g == GROUPS - 1:
+                nc.vector.tensor_add(
+                    out=row_sums[:, PACK - 1 : PACK], in0=vector_sums[:, 0:1], in1=vector_sums[:, 1:2]
+                )
+            return row_sums
 
         def reciprocal_root(row_sums):
             root = stream.tile([P, PACK], F32, tag="root")
@@ -217,11 +231,14 @@ def tile_gcnlayer_pb_t_kernel(tc, h_ln, adj, W2, b2, out):
             )
             return root
 
-        def make_dinv(g, root, row_sums):
+        def find_positive(row_sums):
             positive = stream.tile([P, PACK], F32, tag="positive")
             nc.vector.tensor_scalar(
                 out=positive[:], in0=row_sums[:], scalar1=-1.0, scalar2=None, op0=ALU.is_gt
             )
+            return positive
+
+        def make_dinv(g, root, positive):
             nc.vector.scalar_tensor_tensor(
                 out=dinv[:, g * PACK : (g + 1) * PACK],
                 in0=root[:],
@@ -250,18 +267,29 @@ def tile_gcnlayer_pb_t_kernel(tc, h_ln, adj, W2, b2, out):
         def make_h(g):
             h = psum.tile([P, PACK * FEATS], F32, tag="h")
             for t in range(PACK):
-                h_tile = h[:, t * FEATS : (t + 1) * FEATS]
-                nc.tensor.matmul(h_tile, lhsT=ones, rhs=bias_rows[:], start=True, stop=False)
                 nc.tensor.matmul(
-                    h_tile, lhsT=h_lnT_of[g // 2][:, g % 2, t * P : (t + 1) * P], rhs=w2_sb[:], start=False, stop=True
+                    h[:, t * FEATS : (t + 1) * FEATS],
+                    lhsT=h_lnT_of[g // 2][:, g % 2, t * P : (t + 1) * P],
+                    rhs=w2_sb[:],
+                    start=True,
+                    stop=True,
                 )
+            h_of[g] = h
+
+        def add_bias(g):
+            h = stream.tile([P, PACK, FEATS], F32, tag="h_sb")
+            nc.vector.tensor_add(
+                out=h[:],
+                in0=h_of[g][:].rearrange("p (t f) -> p t f", t=PACK),
+                in1=bias[:].unsqueeze(1).to_broadcast([P, PACK, FEATS]),
+            )
             h_of[g] = h
 
         def group_hs(g):
             hs_grouped = stream.tile([P, FEATS * PACK], BF16, tag="hs_grouped", align_bytes=64)
             nc.vector.tensor_tensor(
                 out=hs_grouped[:].rearrange("q (f t) -> q f t", t=PACK),
-                in0=h_of[g][:].rearrange("q (t f) -> q f t", t=PACK),
+                in0=h_of[g][:].rearrange("q t f -> q f t"),
                 in1=dinv[:, PACK * g : PACK * (g + 1)].unsqueeze(1).to_broadcast([P, FEATS, PACK]),
                 op=ALU.mult,
             )
@@ -279,7 +307,7 @@ def tile_gcnlayer_pb_t_kernel(tc, h_ln, adj, W2, b2, out):
                 s = PACK * g + t
                 nc.scalar.activation(
                     out=acc[:, g, t * FEATS : (t + 1) * FEATS],
-                    in_=h_of[g][:, t * FEATS : (t + 1) * FEATS],
+                    in_=h_of[g][:, t, :],
                     func=ACT.Copy,
                     scale=dinv[:, s : s + 1],
                 )
@@ -334,22 +362,29 @@ def tile_gcnlayer_pb_t_kernel(tc, h_ln, adj, W2, b2, out):
             load(0)
             load(1)
             load(2)
-            warm(16)
+            warm(24)
+            bias_bank = psum.tile([P, BANK], F32, tag="h")
+            nc.tensor.matmul(bias_bank[:, :FEATS], lhsT=ones, rhs=bias_rows[:], start=True, stop=True)
+            nc.scalar.copy(out=bias[:], in_=bias_bank[:, :FEATS])
             for half in range(HALVES):
                 sort(0, half)
-            folding = None
             grouping = None
+            sums_sb = None
             for s in range(TILES):
-                last = [GROUPS - 1]
-                making = last if s == TILES - 1 else [g for g in range(GROUPS - 1) if s == PACK * g + 4]
-                folding_now = [g for g in range(GROUPS - 1) if s == PACK * g + 5]
-                scaling = last if s == TILES - 1 else [g for g in range(GROUPS - 1) if s == PACK * g + 6]
+                last = [GROUPS - 1] if s == TILES - 1 else []
+                making = [g for g in range(GROUPS - 1) if s == PACK * g + 4] + last
+                folding = [g for g in range(GROUPS - 1) if s == PACK * g + 5] + last
+                scaling = [g for g in range(GROUPS - 1) if s == PACK * g + 6] + last
                 finishing = [g for g in range(GROUPS - 1) if s == PACK * g + 7]
                 if s + 3 < TILES:
                     load(s + 3)
                 if s % 8 == 0:
                     load_features(s // 8)
 
+                if last:
+                    sum_rows(s - 1)
+                    sums_sb = copy_sums(GROUPS - 1)
+                    fold_sums(GROUPS - 1, sums_sb)
                 if s + 1 < TILES:
                     sort(s + 1, 0)
                 for g in finishing:
@@ -358,32 +393,42 @@ def tile_gcnlayer_pb_t_kernel(tc, h_ln, adj, W2, b2, out):
                     copy_features(s // 8)
                 turn(s, 0)
                 for g in scaling:
-                    row_sums = row_sums_of(g)
-                    root = reciprocal_root(row_sums)
+                    own = pick_own(g)
                 if s >= 1:
                     quantise(s - 1, 0)
+                for g in scaling:
+                    row_sums = add_own(g, own)
                 if s + 1 < TILES:
                     sort(s + 1, 1)
                 for g in finishing:
                     keep_hs(g)
+                for g in last:
+                    root = reciprocal_root(row_sums)
                 turn(s, 1)
+                for g in scaling:
+                    positive = find_positive(row_sums)
+                    if not last:
+                        root = reciprocal_root(row_sums)
                 if s >= 1:
                     quantise(s - 1, 1)
-                    if s - 1 < FIRST_VECTOR_SUM:
+                    if not last:
                         sum_rows(s - 1)
                         if s % PACK == 0:
-                            folding = copy_sums(s // PACK - 1)
-                for g in folding_now:
-                    fold_sums(g, folding)
+                            sums_sb = copy_sums(s // PACK - 1)
+                if not last:
+                    for g in folding:
+                        fold_sums(g, sums_sb)
                 if s % 8 == 3:
                     turn_features(s // 8)
                 for g in making:
                     make_h(g)
                 for g in scaling:
-                    make_dinv(g, root, row_sums)
-                    grouping = group_hs(g)
+                    add_bias(g)
+                    make_dinv(g, root, positive)
                 collect(work["ready"])
                 work["ready"] = []
+                for g in scaling:
+                    grouping = group_hs(g)
                 multiply(passes_in_step(s))
 
             quantise_hs(GROUPS - 1, grouping)

@@ -53,9 +53,9 @@ def passes_in_step(s):
 def tile_gcnlayer_pb_t_kernel(tc, h_ln, adj, W2, b2, out):
     nc = tc.nc
 
-    adj_tiles = adj.rearrange("(g p e) j -> p g e j", p=P, e=PACK)
-    h_ln_groups = h_ln.rearrange("(g p e) k -> p g (e k)", p=P, e=PACK)
-    out_groups = out.rearrange("(g p e) f -> p g (e f)", p=P, e=PACK)
+    adj_tiles = adj.rearrange("(g m u r e) j -> r m g u e j", m=P // 2, u=2, r=2, e=2)
+    h_ln_groups = h_ln.rearrange("(g m u r e) k -> r m g u (e k)", m=P // 2, u=2, r=2, e=2)
+    out_groups = out.rearrange("(g m u r e) f -> r m g u (e f)", m=P // 2, u=2, r=2, e=2)
 
     with tc.tile_pool(name="keep", bufs=1) as keep, tc.tile_pool(name="stream", bufs=2) as stream, tc.psum_pool(
         name="psum", bufs=1
@@ -118,15 +118,21 @@ def tile_gcnlayer_pb_t_kernel(tc, h_ln, adj, W2, b2, out):
             pieces = 4 if s == 0 else 1
             width = NODES // pieces
             for i in range(pieces):
-                nc.sync.dma_start(
-                    out=rows[:, i * width : (i + 1) * width],
-                    in_=adj_tiles[:, s // PACK, s % PACK, i * width : (i + 1) * width],
-                )
+                for r in range(2):
+                    nc.sync.dma_start(
+                        out=rows[r:P:2, i * width : (i + 1) * width],
+                        in_=adj_tiles[r, :, s // PACK, s % PACK // 2, s % 2, i * width : (i + 1) * width],
+                    )
             rows_of[s] = rows
 
         def load_features(pair):
             features = stream.tile([P, 2, PACK * FEATS], BF16, tag="features", bufs=1)
-            nc.sync.dma_start(out=features[:], in_=h_ln_groups[:, 2 * pair : 2 * pair + 2, :])
+            for r in range(2):
+                for i in range(2):
+                    nc.sync.dma_start(
+                        out=features[r:P:2, i, :].rearrange("m (u x) -> m u x", u=2),
+                        in_=h_ln_groups[r, :, 2 * pair + i, :, :],
+                    )
             features_of[pair] = features
 
         def sort(s, half):
@@ -134,13 +140,13 @@ def tile_gcnlayer_pb_t_kernel(tc, h_ln, adj, W2, b2, out):
             source = rows_of[s][:, half * HALF : (half + 1) * HALF]
             if s < FIRST_VECTOR_SUM:
                 nc.vector.tensor_copy(
-                    out=paired[:].bitcast(F32).rearrange("p (u n) -> p u n", u=2),
-                    in_=source.bitcast(F32).rearrange("p (n u) -> p u n", u=2),
+                    out=paired[:].bitcast(F32).rearrange("p (c u m r) -> p c u m r", c=PASSES_IN_HALF, u=2, r=2),
+                    in_=source.bitcast(F32).rearrange("p (c m u r) -> p c u m r", c=PASSES_IN_HALF, u=2, r=2),
                 )
             else:
                 nc.vector.tensor_scalar(
-                    out=paired[:].rearrange("p (u n e) -> p u n e", u=2, e=2),
-                    in0=source.rearrange("p (n u e) -> p u n e", u=2, e=2),
+                    out=paired[:].rearrange("p (u n x) -> p u n x", u=2, x=4),
+                    in0=source.rearrange("p (n u x) -> p u n x", u=2, x=4),
                     scalar1=1.0,
                     scalar2=None,
                     op0=ALU.mult,
@@ -150,7 +156,7 @@ def tile_gcnlayer_pb_t_kernel(tc, h_ln, adj, W2, b2, out):
             paired_of[s, half] = paired
 
         def turn(s, half):
-            words = paired_of[s, half][:].bitcast(F32).rearrange("p (u n) -> p u n", u=2)
+            words = paired_of[s, half][:].bitcast(F32).rearrange("p (k w) -> p k w", w=P)
             grouped = stream.tile([P, HALF], BF16, tag="grouped", bufs=5, align_bytes=64)
             grouped_words = grouped[:].bitcast(F32).rearrange("q (c i u) -> q c i u", i=P, u=2)
             for b in range(BANKS_IN_HALF):
@@ -158,11 +164,8 @@ def tile_gcnlayer_pb_t_kernel(tc, h_ln, adj, W2, b2, out):
                 bank = psum.tile([P, BANK], F32, tag="turn", bufs=4)
                 for place in range(2 * PASSES_IN_BANK):
                     c, u = first + place // 2, place % 2
-                    nc.tensor.transpose(
-                        bank[:, place * P : (place + 1) * P],
-                        words[:, u, c * P : (c + 1) * P],
-                        ident_f32[:],
-                    )
+                    block = 2 * c + u if s < FIRST_VECTOR_SUM else u * PASSES_IN_HALF + c
+                    nc.tensor.transpose(bank[:, place * P : (place + 1) * P], words[:, block, :], ident_f32[:])
                 nc.scalar.copy(
                     out=grouped_words[:, first : first + PASSES_IN_BANK, :, :],
                     in_=bank[:].rearrange("q (c u i) -> q c i u", c=PASSES_IN_BANK, u=2),
@@ -329,7 +332,10 @@ def tile_gcnlayer_pb_t_kernel(tc, h_ln, adj, W2, b2, out):
             for v, t, c in jobs[work["next"] : work["next"] + count]:
                 g, lo, hi = VISITS[v]
                 if t == 0 and c == lo:
-                    work["bank"] = psum.tile([P, BANK], F32, tag="agg", bufs=2, name="agg")
+                    if hi == PASSES and v % 3 != 0:
+                        work["bank"] = psum.tile([P, BANK], F32, tag="turn", bufs=4, name="agg")
+                    else:
+                        work["bank"] = psum.tile([P, BANK], F32, tag="agg", bufs=2, name="agg")
                 s = PACK * g + t
                 nc.tensor.matmul_mx(
                     out=work["bank"][:, t * FEATS : (t + 1) * FEATS],
@@ -356,7 +362,11 @@ def tile_gcnlayer_pb_t_kernel(tc, h_ln, adj, W2, b2, out):
                             func=ACT.Copy,
                             scale=dinv[:, s : s + 1],
                         )
-                    nc.sync.dma_start(out=out_groups[:, g, :], in_=acc[:, g, :])
+                    for r in range(2):
+                        nc.sync.dma_start(
+                            out=out_groups[r, :, g, :, :],
+                            in_=acc[r:P:2, g, :].rearrange("m (u x) -> m u x", u=2),
+                        )
 
         with tc.manual_schedule():
             load(0)

@@ -25,29 +25,20 @@ BANKS_IN_HALF = PASSES_IN_HALF // PASSES_IN_BANK
 ROWS_IN_CHUNK = P // PACK
 CHUNKS = P // ROWS_IN_CHUNK
 SUMS = CHUNKS * PACK
-SUM_COLS = 8
+SUM_COLS = 14
+FEW_SUM_COLS = 2
+WIDE_TILES = 18
+FIRST_PASSES = 20
+CROWDED = 28
+FILL = 2
 PLANE_STEP = 4
 FIRST_VECTOR_SUM = TILES - 1
 
 BIG = 2.0**60
 
-VISITS = (
-    [(g, 0, 4) for g in range(4)]
-    + [(g, 4, 6) for g in range(4)]
-    + [(g, 0, 6) for g in range(4, 7)]
-    + [(g, 6, 8) for g in range(7)]
-    + [(7, 0, 8)]
-)
+VISITS = ([(g, 0, 4) for g in range(4)] + [(g, 0, 6) for g in range(4, 7)] + [(g, 4, 8) for g in range(4)] + [(g, 6, 8) for g in range(4, 7)] + [(7, 0, 8)])
 
 FLOPS = 2 * NODES * NODES * FEATS + 2 * NODES * FEATS * FEATS
-
-
-def passes_in_step(s):
-    if s < 19:
-        return 0
-    if s < 27:
-        return 8
-    return 16 if s < 29 else 24
 
 
 def tile_gcnlayer_pb_t_kernel(tc, h_ln, adj, W2, b2, out):
@@ -102,7 +93,7 @@ def tile_gcnlayer_pb_t_kernel(tc, h_ln, adj, W2, b2, out):
         bias = keep.tile([P, FEATS], F32)
         first_folded = 2 * SUMS * SUM_COLS
         part_sums = sums[:, :first_folded].rearrange("p (g k e) -> p g k e", g=2, e=SUM_COLS)
-        folded = sums[:, first_folded : first_folded + GROUPS * SUMS].rearrange("p (g k) -> p g k", g=GROUPS)
+        folded = sums[:, first_folded : first_folded + 2 * SUMS].rearrange("p (g k) -> p g k", g=2)
 
         rows_of = {}
         paired_of = {}
@@ -180,17 +171,19 @@ def tile_gcnlayer_pb_t_kernel(tc, h_ln, adj, W2, b2, out):
                 in_=grouped_of[s, half][:],
             )
 
-        def sum_rows(s):
+        def sum_rows(s, fill):
+            cols = SUM_COLS if s < WIDE_TILES else FEW_SUM_COLS
             for chunk in range(CHUNKS):
                 for c in range(PASSES):
                     first_col = (c % PASSES_IN_HALF * P + chunk * ROWS_IN_CHUNK) * PACK
                     nc.tensor.matmul(
-                        part_sums[:, s // PACK % 2, chunk * PACK + s % PACK, :],
+                        part_sums[:, s // PACK % 2, chunk * PACK + s % PACK, :cols],
                         lhsT=grouped_of[s, c // PASSES_IN_HALF][:, first_col : first_col + P],
-                        rhs=ones[:, 0:SUM_COLS],
+                        rhs=ones[:, 0:cols],
                         start=(c == 0),
                         stop=(c == PASSES - 1),
                     )
+                fill()
 
         def copy_sums(g):
             sums_sb = stream.tile([P, SUMS], F32, tag="sums_sb")
@@ -199,7 +192,7 @@ def tile_gcnlayer_pb_t_kernel(tc, h_ln, adj, W2, b2, out):
 
         def fold_sums(g, sums_sb):
             nc.tensor.matmul(
-                folded[:, g, :],
+                folded[:, g % 2, :],
                 lhsT=fold[:].rearrange("k c i -> k (c i)"),
                 rhs=sums_sb[:],
                 start=True,
@@ -209,7 +202,7 @@ def tile_gcnlayer_pb_t_kernel(tc, h_ln, adj, W2, b2, out):
         def pick_own(g):
             own = stream.tile([P, CHUNKS, PACK], F32, tag="own")
             nc.vector.tensor_mul(
-                out=own[:], in0=folded[:, g, :].rearrange("p (c t) -> p c t", c=CHUNKS), in1=own_chunk[:]
+                out=own[:], in0=folded[:, g % 2, :].rearrange("p (c t) -> p c t", c=CHUNKS), in1=own_chunk[:]
             )
             return own
 
@@ -305,8 +298,8 @@ def tile_gcnlayer_pb_t_kernel(tc, h_ln, adj, W2, b2, out):
                 in_=hs_grouped[:],
             )
 
-        def keep_hs(g):
-            for t in range(PACK):
+        def keep_hs(g, tiles):
+            for t in tiles:
                 s = PACK * g + t
                 nc.scalar.activation(
                     out=acc[:, g, t * FEATS : (t + 1) * FEATS],
@@ -372,7 +365,7 @@ def tile_gcnlayer_pb_t_kernel(tc, h_ln, adj, W2, b2, out):
             load(0)
             load(1)
             load(2)
-            warm(24)
+            warm(40)
             bias_bank = psum.tile([P, BANK], F32, tag="h")
             nc.tensor.matmul(bias_bank[:, :FEATS], lhsT=ones, rhs=bias_rows[:], start=True, stop=True)
             nc.scalar.copy(out=bias[:], in_=bias_bank[:, :FEATS])
@@ -386,13 +379,14 @@ def tile_gcnlayer_pb_t_kernel(tc, h_ln, adj, W2, b2, out):
                 folding = [g for g in range(GROUPS - 1) if s == PACK * g + 5] + last
                 scaling = [g for g in range(GROUPS - 1) if s == PACK * g + 6] + last
                 finishing = [g for g in range(GROUPS - 1) if s == PACK * g + 7]
+                ready, work["ready"] = work["ready"], []
                 if s + 3 < TILES:
                     load(s + 3)
                 if s % 8 == 0:
                     load_features(s // 8)
 
                 if last:
-                    sum_rows(s - 1)
+                    sum_rows(s - 1, lambda: None)
                     sums_sb = copy_sums(GROUPS - 1)
                     fold_sums(GROUPS - 1, sums_sb)
                 if s + 1 < TILES:
@@ -410,19 +404,23 @@ def tile_gcnlayer_pb_t_kernel(tc, h_ln, adj, W2, b2, out):
                     row_sums = add_own(g, own)
                 if s + 1 < TILES:
                     sort(s + 1, 1)
-                for g in finishing:
-                    keep_hs(g)
-                for g in last:
+                for g in range(GROUPS - 1):
+                    if 0 <= s - PACK * g - 7 < PACK:
+                        keep_hs(g, [s - PACK * g - 7])
+                for g in scaling:
                     root = reciprocal_root(row_sums)
                 turn(s, 1)
                 for g in scaling:
                     positive = find_positive(row_sums)
-                    if not last:
-                        root = reciprocal_root(row_sums)
                 if s >= 1:
                     quantise(s - 1, 1)
                     if not last:
-                        sum_rows(s - 1)
+                        if s < FIRST_PASSES:
+                            sum_rows(s - 1, lambda: warm(1))
+                        elif s < CROWDED:
+                            sum_rows(s - 1, lambda: multiply(FILL))
+                        else:
+                            sum_rows(s - 1, lambda: multiply(4))
                         if s % PACK == 0:
                             sums_sb = copy_sums(s // PACK - 1)
                 if not last:
@@ -435,16 +433,21 @@ def tile_gcnlayer_pb_t_kernel(tc, h_ln, adj, W2, b2, out):
                 for g in scaling:
                     add_bias(g)
                     make_dinv(g, root, positive)
-                collect(work["ready"])
-                work["ready"] = []
+                collect(ready)
                 for g in scaling:
                     grouping = group_hs(g)
-                multiply(passes_in_step(s))
+                if s == 0:
+                    warm(CHUNKS * FILL)
+                if s == TILES - 1:
+                    multiply(24)
 
             quantise_hs(GROUPS - 1, grouping)
-            keep_hs(GROUPS - 1)
+            keep_hs(GROUPS - 2, range(1, PACK))
+            keep_hs(GROUPS - 1, range(PACK))
             for half in range(HALVES):
                 quantise(TILES - 1, half)
+            collect(work["ready"])
+            work["ready"] = []
             for v in range(jobs[work["next"]][0], len(VISITS)):
                 multiply(len([1 for job in jobs[work["next"] :] if job[0] == v]))
                 collect(work["ready"])

import concourse.mybir as mybir
from concourse.masks import make_identity

F32 = mybir.dt.float32
BF16 = mybir.dt.bfloat16
U32 = mybir.dt.uint32
U8 = mybir.dt.uint8
FP8X4 = mybir.dt.float8_e4m3fn_x4
ALU = mybir.AluOpType
ACT = mybir.ActivationFunctionType

P = 128
NODES = 4096
FEATS = 128
TILES = NODES // P
PACK = 4
GROUPS = TILES // PACK
PASSES = GROUPS
BANK = 512
HALVES = 2
HALF = NODES // HALVES
PASSES_IN_HALF = PASSES // HALVES
PASSES_IN_BANK = 2
BANKS_IN_HALF = PASSES_IN_HALF // PASSES_IN_BANK
ROWS_IN_CHUNK = P // PACK
CHUNKS = P // ROWS_IN_CHUNK
SUMS = CHUNKS * PACK
SUM_COLS = 14
FEW_SUM_COLS = 2
WIDE_TILES = 18
FIRST_PASSES = 20
CROWDED = 28
FILL = 2
PLANE_STEP = 4
FIRST_VECTOR_SUM = TILES - 1

BIG = 2.0**60

VISITS = ([(g, 0, 4) for g in range(4)] + [(g, 0, 6) for g in range(4, 7)] + [(g, 4, 8) for g in range(4)] + [(g, 6, 8) for g in range(4, 7)] + [(7, 0, 8)])

FLOPS = 2 * NODES * NODES * FEATS + 2 * NODES * FEATS * FEATS


def tile_gcnlayer_pb_t_kernel(tc, h_ln, adj, W2, b2, out):
    nc = tc.nc

    adj_tiles = adj.rearrange("(g m u r e) j -> r m g u e j", m=P // 2, u=2, r=2, e=2)
    h_ln_groups = h_ln.rearrange("(g m u r e) k -> r m g u (e k)", m=P // 2, u=2, r=2, e=2)
    out_groups = out.rearrange("(g m u r e) f -> r m g u (e f)", m=P // 2, u=2, r=2, e=2)

    with tc.tile_pool(name="keep", bufs=1) as keep, tc.tile_pool(name="stream", bufs=2) as stream, tc.psum_pool(
        name="psum", bufs=1
    ) as psum:
        ident_f32 = keep.tile([P, P], F32)
        make_identity(nc, ident_f32[:])
        ident_bf16 = keep.tile([P, P], BF16)
        make_identity(nc, ident_bf16[:])
        w2_sb = keep.tile([FEATS, FEATS], BF16)
        nc.scalar.dma_start(out=w2_sb[:], in_=W2)
        bias_rows = keep.tile([P, FEATS], BF16)
        nc.vector.memset(bias_rows[:], 0.0)
        nc.scalar.dma_start(out=bias_rows[0:1, :], in_=b2.rearrange("(o f) -> o f", o=1))
        warm_values = keep.tile([P, P * PACK], BF16, align_bytes=64)
        nc.vector.memset(warm_values[:], 1.0)
        ones = warm_values[:, 0:P]
        one_column = keep.tile([P, 1], F32)
        nc.vector.memset(one_column[:], 1.0)
        warm_codes = keep.tile([P, P], U32, align_bytes=64)
        warm_scales = keep.tile([P, P], U8, align_bytes=64)
        nc.vector.quantize_mx(out=warm_codes[:].bitcast(FP8X4), scales=warm_scales[:], in_=warm_values[:])
        fold = keep.tile([P, CHUNKS, ROWS_IN_CHUNK], F32)
        own_chunk = keep.tile([P, CHUNKS, PACK], F32)
        nc.gpsimd.memset(own_chunk[:], 0.0)
        for chunk in range(CHUNKS):
            nc.vector.tensor_reduce(
                out=fold[:, chunk, :],
                in_=ident_f32[:].rearrange("k (i t) -> k i t", t=PACK),
                axis=mybir.AxisListType.X,
                op=ALU.add,
            )
            nc.gpsimd.memset(own_chunk[chunk * ROWS_IN_CHUNK : (chunk + 1) * ROWS_IN_CHUNK, chunk, :], 1.0)
        table_warmer = keep.tile([P, 1], F32)
        nc.scalar.activation(out=table_warmer[:], in_=one_column[:], func=ACT.Abs_reciprocal_sqrt)

        adj_codes = keep.tile([P, TILES, PASSES * P], U32, align_bytes=64)
        adj_planes = keep.tile([P, GROUPS, PASSES * P], U8, align_bytes=64)
        hs_codes = keep.tile([P, PASSES * FEATS], U32, align_bytes=64)
        hs_scales = keep.tile([P, PASSES * FEATS], U8, align_bytes=64)
        acc = keep.tile([P, GROUPS, PACK * FEATS], F32)
        dinv = keep.tile([P, TILES], F32)
        vector_sums = keep.tile([P, HALVES], F32)
        sums = psum.tile([P, BANK], F32, tag="sums")
        bias = keep.tile([P, FEATS], F32)
        first_folded = 2 * SUMS * SUM_COLS
        part_sums = sums[:, :first_folded].rearrange("p (g k e) -> p g k e", g=2, e=SUM_COLS)
        folded = sums[:, first_folded : first_folded + 2 * SUMS].rearrange("p (g k) -> p g k", g=2)

        rows_of = {}
        paired_of = {}
        grouped_of = {}
        features_of = {}
        h_lnT_of = {}
        h_of = {}
        work = {"next": 0, "bank": None, "ready": []}
        jobs = [(v, t, c) for v, (g, lo, hi) in enumerate(VISITS) for t in range(PACK) for c in range(lo, hi)]

        def load(s):
            rows = stream.tile([P, NODES], BF16, tag="rows", bufs=3)
            pieces = 4 if s == 0 else 1
            width = NODES // pieces
            for i in range(pieces):
                for r in range(2):
                    nc.sync.dma_start(
                        out=rows[r:P:2, i * width : (i + 1) * width],
                        in_=adj_tiles[r, :, s // PACK, s % PACK // 2, s % 2, i * width : (i + 1) * width],
                    )
            rows_of[s] = rows

        def load_features(pair):
            features = stream.tile([P, 2, PACK * FEATS], BF16, tag="features", bufs=1)
            for r in range(2):
                for i in range(2):
                    nc.sync.dma_start(
                        out=features[r:P:2, i, :].rearrange("m (u x) -> m u x", u=2),
                        in_=h_ln_groups[r, :, 2 * pair + i, :, :],
                    )
            features_of[pair] = features

        def sort(s, half):
            paired = stream.tile([P, HALF], BF16, tag="paired", bufs=4)
            source = rows_of[s][:, half * HALF : (half + 1) * HALF]
            if s < FIRST_VECTOR_SUM:
                nc.vector.tensor_copy(
                    out=paired[:].bitcast(F32).rearrange("p (c u m r) -> p c u m r", c=PASSES_IN_HALF, u=2, r=2),
                    in_=source.bitcast(F32).rearrange("p (c m u r) -> p c u m r", c=PASSES_IN_HALF, u=2, r=2),
                )
            else:
                nc.vector.tensor_scalar(
                    out=paired[:].rearrange("p (u n x) -> p u n x", u=2, x=4),
                    in0=source.rearrange("p (n u x) -> p u n x", u=2, x=4),
                    scalar1=1.0,
                    scalar2=None,
                    op0=ALU.mult,
                    op1=ALU.add,
                    accum_out=vector_sums[:, half : half + 1],
                )
            paired_of[s, half] = paired

        def turn(s, half):
            words = paired_of[s, half][:].bitcast(F32).rearrange("p (k w) -> p k w", w=P)
            grouped = stream.tile([P, HALF], BF16, tag="grouped", bufs=5, align_bytes=64)
            grouped_words = grouped[:].bitcast(F32).rearrange("q (c i u) -> q c i u", i=P, u=2)
            for b in range(BANKS_IN_HALF):
                first = b * PASSES_IN_BANK
                bank = psum.tile([P, BANK], F32, tag="turn", bufs=4)
                for place in range(2 * PASSES_IN_BANK):
                    c, u = first + place // 2, place % 2
                    block = 2 * c + u if s < FIRST_VECTOR_SUM else u * PASSES_IN_HALF + c
                    nc.tensor.transpose(bank[:, place * P : (place + 1) * P], words[:, block, :], ident_f32[:])
                nc.scalar.copy(
                    out=grouped_words[:, first : first + PASSES_IN_BANK, :, :],
                    in_=bank[:].rearrange("q (c u i) -> q c i u", c=PASSES_IN_BANK, u=2),
                )
            grouped_of[s, half] = grouped

        def quantise(s, half):
            cols = slice(half * PASSES_IN_HALF * P, (half + 1) * PASSES_IN_HALF * P)
            nc.vector.quantize_mx(
                out=adj_codes[:, s, cols].bitcast(FP8X4),
                scales=adj_planes[PLANE_STEP * (s % PACK) : P, s // PACK, cols],
                in_=grouped_of[s, half][:],
            )

        def sum_rows(s, fill):
            cols = SUM_COLS if s < WIDE_TILES else FEW_SUM_COLS
            for chunk in range(CHUNKS):
                for c in range(PASSES):
                    first_col = (c % PASSES_IN_HALF * P + chunk * ROWS_IN_CHUNK) * PACK
                    nc.tensor.matmul(
                        part_sums[:, s // PACK % 2, chunk * PACK + s % PACK, :cols],
                        lhsT=grouped_of[s, c // PASSES_IN_HALF][:, first_col : first_col + P],
                        rhs=ones[:, 0:cols],
                        start=(c == 0),
                        stop=(c == PASSES - 1),
                    )
                fill()

        def copy_sums(g):
            sums_sb = stream.tile([P, SUMS], F32, tag="sums_sb")
            nc.scalar.copy(out=sums_sb[:], in_=part_sums[:, g % 2, :, 0])
            return sums_sb

        def fold_sums(g, sums_sb):
            nc.tensor.matmul(
                folded[:, g % 2, :],
                lhsT=fold[:].rearrange("k c i -> k (c i)"),
                rhs=sums_sb[:],
                start=True,
                stop=True,
            )

        def pick_own(g):
            own = stream.tile([P, CHUNKS, PACK], F32, tag="own")
            nc.vector.tensor_mul(
                out=own[:], in0=folded[:, g % 2, :].rearrange("p (c t) -> p c t", c=CHUNKS), in1=own_chunk[:]
            )
            return own

        def add_own(g, own):
            row_sums = stream.tile([P, PACK], F32, tag="row_sums")
            nc.vector.tensor_reduce(
                out=row_sums[:],
                in_=own[:].rearrange("p c t -> p t c"),
                axis=mybir.AxisListType.X,
                op=ALU.add,
            )
            if g == GROUPS - 1:
                nc.vector.tensor_add(
                    out=row_sums[:, PACK - 1 : PACK], in0=vector_sums[:, 0:1], in1=vector_sums[:, 1:2]
                )
            return row_sums

        def reciprocal_root(row_sums):
            root = stream.tile([P, PACK], F32, tag="root")
            nc.scalar.activation(
                out=root[:], in_=row_sums[:], func=ACT.Abs_reciprocal_sqrt, bias=one_column[:]
            )
            return root

        def find_positive(row_sums):
            positive = stream.tile([P, PACK], F32, tag="positive")
            nc.vector.tensor_scalar(
                out=positive[:], in0=row_sums[:], scalar1=-1.0, scalar2=None, op0=ALU.is_gt
            )
            return positive

        def make_dinv(g, root, positive):
            nc.vector.scalar_tensor_tensor(
                out=dinv[:, g * PACK : (g + 1) * PACK],
                in0=root[:],
                scalar=BIG,
                in1=positive[:],
                op0=ALU.min,
                op1=ALU.mult,
            )

        def turn_features(pair):
            bank = psum.tile([P, 2, PACK * P], BF16, tag="h")
            for i in range(2):
                for t in range(PACK):
                    nc.tensor.transpose(
                        bank[:, i, t * P : (t + 1) * P],
                        features_of[pair][:, i, t * FEATS : (t + 1) * FEATS],
                        ident_bf16[:],
                    )
            h_lnT_of[pair] = bank

        def copy_features(pair):
            h_lnT = stream.tile([P, 2, PACK * P], BF16, tag="h_lnT", bufs=1)
            nc.scalar.copy(out=h_lnT[:], in_=h_lnT_of[pair][:])
            h_lnT_of[pair] = h_lnT

        def make_h(g):
            h = psum.tile([P, PACK * FEATS], F32, tag="h")
            for t in range(PACK):
                nc.tensor.matmul(
                    h[:, t * FEATS : (t + 1) * FEATS],
                    lhsT=h_lnT_of[g // 2][:, g % 2, t * P : (t + 1) * P],
                    rhs=w2_sb[:],
                    start=True,
                    stop=True,
                )
            h_of[g] = h

        def add_bias(g):
            h = stream.tile([P, PACK, FEATS], F32, tag="h_sb")
            nc.vector.tensor_add(
                out=h[:],
                in0=h_of[g][:].rearrange("p (t f) -> p t f", t=PACK),
                in1=bias[:].unsqueeze(1).to_broadcast([P, PACK, FEATS]),
            )
            h_of[g] = h

        def group_hs(g):
            hs_grouped = stream.tile([P, FEATS * PACK], BF16, tag="hs_grouped", align_bytes=64)
            nc.vector.tensor_tensor(
                out=hs_grouped[:].rearrange("q (f t) -> q f t", t=PACK),
                in0=h_of[g][:].rearrange("q t f -> q f t"),
                in1=dinv[:, PACK * g : PACK * (g + 1)].unsqueeze(1).to_broadcast([P, FEATS, PACK]),
                op=ALU.mult,
            )
            return hs_grouped

        def quantise_hs(g, hs_grouped):
            nc.vector.quantize_mx(
                out=hs_codes[:, g * FEATS : (g + 1) * FEATS].bitcast(FP8X4),
                scales=hs_scales[:, g * FEATS : (g + 1) * FEATS],
                in_=hs_grouped[:],
            )

        def keep_hs(g, tiles):
            for t in tiles:
                s = PACK * g + t
                nc.scalar.activation(
                    out=acc[:, g, t * FEATS : (t + 1) * FEATS],
                    in_=h_of[g][:, t, :],
                    func=ACT.Copy,
                    scale=dinv[:, s : s + 1],
                )

        def warm(count):
            bank = psum.tile([P, BANK], F32, tag="agg", bufs=2)
            for i in range(count):
                nc.tensor.matmul_mx(
                    out=bank[:, 0:P],
                    lhsT=warm_codes[:].bitcast(FP8X4),
                    lhsT_scale=warm_scales[:],
                    rhs=warm_codes[:].bitcast(FP8X4),
                    rhs_scale=warm_scales[:],
                    start=True,
                    stop=True,
                )

        def multiply(count):
            for v, t, c in jobs[work["next"] : work["next"] + count]:
                g, lo, hi = VISITS[v]
                if t == 0 and c == lo:
                    if hi == PASSES and v % 3 != 0:
                        work["bank"] = psum.tile([P, BANK], F32, tag="turn", bufs=4, name="agg")
                    else:
                        work["bank"] = psum.tile([P, BANK], F32, tag="agg", bufs=2, name="agg")
                s = PACK * g + t
                nc.tensor.matmul_mx(
                    out=work["bank"][:, t * FEATS : (t + 1) * FEATS],
                    lhsT=adj_codes[:, s, c * P : (c + 1) * P].bitcast(FP8X4),
                    lhsT_scale=adj_planes[PLANE_STEP * t : P, g, c * P : (c + 1) * P],
                    rhs=hs_codes[:, c * FEATS : (c + 1) * FEATS].bitcast(FP8X4),
                    rhs_scale=hs_scales[:, c * FEATS : (c + 1) * FEATS],
                    start=(c == lo),
                    stop=(c == hi - 1),
                )
                if t == PACK - 1 and c == hi - 1:
                    work["ready"].append((g, hi, work["bank"]))
            work["next"] += count

        def collect(visits):
            for g, hi, bank in visits:
                nc.vector.tensor_add(out=acc[:, g, :], in0=bank[:], in1=acc[:, g, :])
                if hi == PASSES:
                    for t in range(PACK):
                        s = PACK * g + t
                        nc.scalar.activation(
                            out=acc[:, g, t * FEATS : (t + 1) * FEATS],
                            in_=acc[:, g, t * FEATS : (t + 1) * FEATS],
                            func=ACT.Copy,
                            scale=dinv[:, s : s + 1],
                        )
                    for r in range(2):
                        nc.sync.dma_start(
                            out=out_groups[r, :, g, :, :],
                            in_=acc[r:P:2, g, :].rearrange("m (u x) -> m u x", u=2),
                        )

        with tc.manual_schedule():
            load(0)
            load(1)
            load(2)
            warm(40)
            bias_bank = psum.tile([P, BANK], F32, tag="h")
            nc.tensor.matmul(bias_bank[:, :FEATS], lhsT=ones, rhs=bias_rows[:], start=True, stop=True)
            nc.scalar.copy(out=bias[:], in_=bias_bank[:, :FEATS])
            for half in range(HALVES):
                sort(0, half)
            grouping = None
            sums_sb = None
            for s in range(TILES):
                last = [GROUPS - 1] if s == TILES - 1 else []
                making = [g for g in range(GROUPS - 1) if s == PACK * g + 4] + last
                folding = [g for g in range(GROUPS - 1) if s == PACK * g + 5] + last
                scaling = [g for g in range(GROUPS - 1) if s == PACK * g + 6] + last
                finishing = [g for g in range(GROUPS - 1) if s == PACK * g + 7]
                ready, work["ready"] = work["ready"], []
                if s + 3 < TILES:
                    load(s + 3)
                if s % 8 == 0:
                    load_features(s // 8)

                if last:
                    sum_rows(s - 1, lambda: None)
                    sums_sb = copy_sums(GROUPS - 1)
                    fold_sums(GROUPS - 1, sums_sb)
                if s + 1 < TILES:
                    sort(s + 1, 0)
                for g in finishing:
                    quantise_hs(g, grouping)
                if s % 8 == 4:
                    copy_features(s // 8)
                turn(s, 0)
                for g in scaling:
                    own = pick_own(g)
                if s >= 1:
                    quantise(s - 1, 0)
                for g in scaling:
                    row_sums = add_own(g, own)
                if s + 1 < TILES:
                    sort(s + 1, 1)
                for g in range(GROUPS - 1):
                    if 0 <= s - PACK * g - 7 < PACK:
                        keep_hs(g, [s - PACK * g - 7])
                for g in scaling:
                    root = reciprocal_root(row_sums)
                turn(s, 1)
                for g in scaling:
                    positive = find_positive(row_sums)
                if s >= 1:
                    quantise(s - 1, 1)
                    if not last:
                        if s < FIRST_PASSES:
                            sum_rows(s - 1, lambda: warm(1))
                        elif s < CROWDED:
                            sum_rows(s - 1, lambda: multiply(FILL))
                        else:
                            sum_rows(s - 1, lambda: multiply(4))
                        if s % PACK == 0:
                            sums_sb = copy_sums(s // PACK - 1)
                if not last:
                    for g in folding:
                        fold_sums(g, sums_sb)
                if s % 8 == 3:
                    turn_features(s // 8)
                for g in making:
                    make_h(g)
                for g in scaling:
                    add_bias(g)
                    make_dinv(g, root, positive)
                collect(ready)
                for g in scaling:
                    grouping = group_hs(g)
                if s == 0:
                    warm(CHUNKS * FILL)
                if s == TILES - 1:
                    multiply(24)

            quantise_hs(GROUPS - 1, grouping)
            keep_hs(GROUPS - 2, range(1, PACK))
            keep_hs(GROUPS - 1, range(PACK))
            for half in range(HALVES):
                quantise(TILES - 1, half)
            collect(work["ready"])
            work["ready"] = []
            for v in range(jobs[work["next"]][0], len(VISITS)):
                multiply(len([1 for job in jobs[work["next"] :] if job[0] == v]))
                collect(work["ready"])
                work["ready"] = []
